import numpy as np
import ml_dtypes


def mxq(x, axis, fmt="e4m3"):
    dtype, down = {"e4m3": (ml_dtypes.float8_e4m3fn, 7), "e5m2": (ml_dtypes.float8_e5m2, 14)}[fmt]
    v = np.moveaxis(np.asarray(x, np.float32).astype(ml_dtypes.bfloat16).astype(np.float64), axis, -1)
    blocks = v.reshape(v.shape[:-1] + (-1, 32))
    amax = np.abs(blocks).max(-1, keepdims=True)
    byte = np.maximum(np.where(amax > 0, np.frexp(amax)[1] - 1 + 127, 0) - down, 1)
    scale = np.exp2(byte - 127.0)
    codes = (blocks / scale).astype(np.float32).astype(dtype).astype(np.float64)
    return np.moveaxis((codes * scale).reshape(v.shape), -1, axis)


WIDE = False


def mx_kscale(k):
    if not WIDE:
        return np.ones(k)
    levels = np.array([10, -10, 5, -5, 0])
    a = np.random.permutation(np.resize(levels, k // 512 * 4)).reshape(k // 512, 4)
    idx = np.arange(k)
    return np.exp2(a[idx // 512, idx % 128 // 32])


BF16 = ml_dtypes.bfloat16


def bf(x):
    return np.asarray(x, np.float32).astype(BF16)


def f64(x):
    return np.asarray(x).astype(np.float64)


B, N, DIN, DS, GE, HID, NS, KC = 1, 2048, 128, 64, 8, 32, 2, 3
DO = DS
C = DIN + DS + DS
F = NS * KC * C
SHARP = 4.0


def sigmoid(v):
    return 1.0 / (1.0 + np.exp(-v))


def softmax(v):
    e = np.exp(v - v.max(-1, keepdims=True))
    return e / e.sum(-1, keepdims=True)


def setup_inputs():
    s = mx_kscale(N)
    adj = softmax(SHARP * np.random.standard_normal((NS, B, N, N)))
    return {"xg_gate": bf(np.random.standard_normal((B, N, F)) * 0.8),
            "gate_w_z": bf(np.random.standard_normal((F, DO + DO)) * 1.5 / np.sqrt(F)),
            "gate_b_z": bf(np.random.standard_normal(DO + DO) * 0.5),
            "xt": bf(np.random.standard_normal((B, N, DIN)) / s[:, None]),
            "state1": bf(np.random.standard_normal((B, N, DS)) / s[:, None]),
            "state2": bf(np.random.standard_normal((B, N, DS)) / s[:, None]),
            "supports": bf(adj * s / s[:, None])}


def reference(xg_gate, gate_w_z, gate_b_z, xt, state1, state2, supports):
    z = sigmoid(f64(xg_gate) @ f64(gate_w_z) + f64(gate_b_z))
    cand = np.concatenate([f64(xt), z[..., :DO] * f64(state1), z[..., DO:] * f64(state2)], axis=-1)
    cq = mxq(cand, 1, "e4m3")
    terms = []
    for i in range(NS):
        aq = mxq(f64(supports)[i], 2, "e4m3")
        t_prev, t_cur = cand, aq @ cq
        ts = [t_prev, t_cur]
        for _ in range(KC - len(ts)):
            t_prev, t_cur = t_cur, 2.0 * (aq @ mxq(t_cur, 1, "e4m3")) - t_prev
            ts.append(t_cur)
        terms.extend(ts)
    return np.concatenate(terms, axis=-1)

@@ -1,0 +1,265 @@
+from contextlib import ExitStack
+
+import concourse.mybir as mybir
+from concourse.masks import make_identity
+
+F32 = mybir.dt.float32
+BF16 = mybir.dt.bfloat16
+U32 = mybir.dt.uint32
+U8 = mybir.dt.uint8
+FP8X4 = mybir.dt.float8_e4m3fn_x4
+ACT = mybir.ActivationFunctionType
+ALU = mybir.AluOpType
+
+P = 128
+PAIR = 2
+PACK = 4
+NODES = 2048
+GROUP = P * PAIR
+N_GROUPS = NODES // GROUP
+N_PASSES = NODES // (P * PACK)
+GROUPS_PER_PASS = P * PACK // GROUP
+SUPPORTS = 2
+F_GATE = 1536
+F_CHUNKS = F_GATE // GROUP
+D_IN = 128
+D_STATE = 64
+C = D_IN + 2 * D_STATE
+BANK = 512
+PER_BANK = BANK // P
+TERMS = 3
+
+FLOPS = 2 * NODES * F_GATE * P + 2 * SUPPORTS * 2 * NODES * NODES * C
+
+
+def tile_dgggl_pa_kernel(tc, xg_gate, gate_w_z, gate_b_z, xt, state1, state2, supports, out):
+    nc = tc.nc
+
+    xg_groups = xg_gate[0].rearrange("(g r e) f -> g r (e f)", r=P, e=PAIR)
+    out_groups = out[0].rearrange("(g r e) f -> g r e f", r=P, e=PAIR)
+
+    with ExitStack() as ctx:
+        keep = ctx.enter_context(tc.tile_pool(name="keep", bufs=1))
+        stream = ctx.enter_context(tc.tile_pool(name="stream", bufs=2))
+        psum = ctx.enter_context(tc.psum_pool(name="psum", bufs=8))
+        ctx.enter_context(tc.manual_schedule())
+
+        ident = keep.tile([P, P], F32)
+        make_identity(nc, ident[:])
+        table_warmer = keep.tile([P, 1], F32)
+        nc.scalar.activation(out=table_warmer[:], in_=ident[:, 0:1], func=ACT.Sigmoid)
+
+        xg_raw = []
+        a_raw = [[], []]
+
+        def load_xg(k):
+            raw = stream.tile([P, PAIR * F_GATE], BF16, name="xg_raw_%d" % k, tag="xg_raw", bufs=3)
+            nc.sync.dma_start(out=raw[:], in_=xg_groups[k])
+            xg_raw.append(raw)
+
+        def load_a(i, b):
+            raw = stream.tile([P, PAIR * NODES], BF16, name="a_raw_%d_%d" % (i, b), tag="a_raw", bufs=4)
+            a_groups = supports[i, 0].rearrange("(g r e) m -> g r (e m)", r=P, e=PAIR)
+            nc.sync.dma_start(out=raw[:], in_=a_groups[b])
+            a_raw[i].append(raw)
+
+        load_xg(0)
+        w_sb = keep.tile([P, F_CHUNKS, PAIR * P], BF16)
+        nc.sync.dma_start(out=w_sb[:], in_=gate_w_z.rearrange("(j q e) c -> q j (e c)", q=P, e=PAIR))
+        bias_bf = keep.tile([P, 1], BF16)
+        with nc.allow_non_contiguous_dma(reason="128 bias values, one to a partition"):
+            nc.sync.dma_start(out=bias_bf[:], in_=gate_b_z.rearrange("(c o) -> c o", o=1))
+        load_a(0, 0)
+        xt_sb = keep.tile([P, N_GROUPS, PAIR * D_IN], BF16)
+        nc.sync.dma_start(out=xt_sb[:], in_=xt[0].rearrange("(g r e) c -> r g (e c)", r=P, e=PAIR))
+        s1_sb = keep.tile([P, N_GROUPS, PAIR * D_STATE], BF16)
+        nc.sync.dma_start(out=s1_sb[:], in_=state1[0].rearrange("(g r e) c -> r g (e c)", r=P, e=PAIR))
+        s2_sb = keep.tile([P, N_GROUPS, PAIR * D_STATE], BF16)
+        nc.sync.dma_start(out=s2_sb[:], in_=state2[0].rearrange("(g r e) c -> r g (e c)", r=P, e=PAIR))
+        for k in range(1, N_GROUPS):
+            load_xg(k)
+            load_a(0, k)
+        for b in range(N_GROUPS):
+            load_a(1, b)
+
+        bias = keep.tile([P, 1], F32)
+        nc.vector.tensor_copy(out=bias[:], in_=bias_bf[:])
+
+        cand = keep.tile([P, N_GROUPS * PAIR, C], F32)
+        a_codes = [[], []]
+        a_scales = [[], []]
+        for i in range(SUPPORTS):
+            for b in range(N_GROUPS):
+                a_codes[i].append(
+                    keep.tile([P, PAIR * N_PASSES * P], U32, name="a_codes_%d_%d" % (i, b), align_bytes=64)
+                )
+                a_scales[i].append(
+                    keep.tile([P, PAIR * N_PASSES * P], U8, name="a_scales_%d_%d" % (i, b), align_bytes=64)
+                )
+        cand_codes = keep.tile([P, N_PASSES, C], U32, align_bytes=64)
+        cand_scales = keep.tile([P, N_PASSES, C], U8, align_bytes=64)
+        t1_codes = []
+        t1_scales = []
+        for i in range(SUPPORTS):
+            t1_codes.append(keep.tile([P, N_PASSES, C], U32, name="t1_codes_%d" % i, align_bytes=64))
+            t1_scales.append(keep.tile([P, N_PASSES, C], U8, name="t1_scales_%d" % i, align_bytes=64))
+
+        def empty_bank(position, run, dst, src):
+            if position == run - 1:
+                nc.vector.tensor_copy(out=dst, in_=src)
+            else:
+                nc.scalar.copy(out=dst, in_=src)
+
+        def transpose_xg_group(k):
+            words = xg_raw[k][:].bitcast(F32)
+            xg_t = stream.tile([P, F_CHUNKS * GROUP], F32, name="xg_t", tag="xg_t")
+            n_banks = F_CHUNKS * PAIR // PER_BANK
+            for bank_no in range(n_banks):
+                bank = psum.tile([P, BANK], F32, name="bank", tag="bank")
+                for s in range(PER_BANK):
+                    j, e = divmod(bank_no * PER_BANK + s, PAIR)
+                    col = (e * F_CHUNKS + j) * P
+                    nc.tensor.transpose(bank[:, s * P : (s + 1) * P], words[:, col : col + P], ident[:])
+                empty_bank(bank_no, n_banks, xg_t[:, bank_no * BANK : (bank_no + 1) * BANK], bank[:])
+            return xg_t
+
+        def gate_matmuls(xg_t):
+            halves = xg_t[:].bitcast(BF16).rearrange("p (j n e) -> p j n e", j=F_CHUNKS, e=PAIR)
+            acc = psum.tile([P, BANK], F32, name="bank", tag="bank")
+            for j in range(F_CHUNKS):
+                for e in range(PAIR):
+                    nc.tensor.matmul(
+                        out=acc[:, 0:GROUP],
+                        lhsT=w_sb[:, j, e * P : (e + 1) * P],
+                        rhs=halves[:, j, :, e],
+                        start=(j == 0 and e == 0),
+                        stop=(j == F_CHUNKS - 1 and e == PAIR - 1),
+                    )
+            z_t = stream.tile([P, GROUP], F32, name="z_t", tag="z_t")
+            nc.scalar.activation(out=z_t[:], in_=acc[:, 0:GROUP], func=ACT.Sigmoid, bias=bias[:, 0:1], scale=1.0)
+            return z_t
+
+        def quantise_rows(rows, codes, scales, g):
+            grouped = stream.tile([P, C * PACK], BF16, name="rows_grouped", tag="rows_grouped", align_bytes=64)
+            nc.vector.tensor_copy(
+                out=grouped[:].rearrange("p (c t) -> p c t", t=PACK), in_=rows.rearrange("p t c -> p c t")
+            )
+            nc.vector.quantize_mx(out=codes[:, g, :].bitcast(FP8X4), scales=scales[:, g, :], in_=grouped[:])
+
+        def finish_cand(k, z_t):
+            bank = psum.tile([P, BANK], F32, name="bank", tag="bank")
+            for e in range(PAIR):
+                nc.tensor.transpose(bank[:, e * P : (e + 1) * P], z_t[:, e * P : (e + 1) * P], ident[:])
+            z = bank[:, 0:GROUP].rearrange("p (e c) -> p e c", e=PAIR)
+            rows = cand[:, k * PAIR : (k + 1) * PAIR, :]
+            nc.scalar.copy(out=rows[:, :, 0:D_IN], in_=xt_sb[:, k, :].rearrange("p (e c) -> p e c", e=PAIR))
+            nc.vector.tensor_tensor(
+                out=rows[:, :, D_IN : D_IN + D_STATE],
+                in0=z[:, :, 0:D_STATE],
+                in1=s1_sb[:, k, :].rearrange("p (e c) -> p e c", e=PAIR),
+                op=ALU.mult,
+            )
+            nc.vector.tensor_tensor(
+                out=rows[:, :, D_IN + D_STATE : C],
+                in0=z[:, :, D_STATE : 2 * D_STATE],
+                in1=s2_sb[:, k, :].rearrange("p (e c) -> p e c", e=PAIR),
+                op=ALU.mult,
+            )
+            for i in range(SUPPORTS):
+                nc.gpsimd.dma_start(out=out_groups[k][:, :, i * TERMS * C : i * TERMS * C + C], in_=rows)
+            g, u = divmod(k, GROUPS_PER_PASS)
+            if u == GROUPS_PER_PASS - 1:
+                quantise_rows(cand[:, g * PACK : (g + 1) * PACK, :], cand_codes, cand_scales, g)
+
+        a_grouped = {}
+
+        def quantise_a_group(i, b):
+            nc.vector.quantize_mx(
+                out=a_codes[i][b][:].bitcast(FP8X4), scales=a_scales[i][b][:], in_=a_grouped[(i, b)][:]
+            )
+
+        def transpose_a_group(i, b):
+            words = a_raw[i][b][:].bitcast(F32)
+            grouped = stream.tile([P, PAIR * NODES], BF16, name="a_grouped", tag="a_grouped", align_bytes=64)
+            grouped_words = grouped[:].bitcast(F32).rearrange("p (x r u) -> p x r u", r=P, u=PAIR)
+            n_banks = NODES // BANK
+            for bank_no in range(n_banks):
+                bank = psum.tile([P, BANK], F32, name="bank", tag="bank")
+                for s in range(PER_BANK):
+                    col = (bank_no * PER_BANK + s) * P
+                    nc.tensor.transpose(bank[:, s * P : (s + 1) * P], words[:, col : col + P], ident[:])
+                empty_bank(
+                    bank_no,
+                    n_banks,
+                    grouped_words[:, bank_no * PAIR : (bank_no + 1) * PAIR, :, :],
+                    bank[:].rearrange("p (x u r) -> p x r u", u=PAIR, r=P),
+                )
+            a_grouped[(i, b)] = grouped
+            if (i, b) != (0, 0):
+                before_i, before_b = divmod(i * N_GROUPS + b - 1, N_GROUPS)
+                quantise_a_group(before_i, before_b)
+
+        def product_with_a(i, b, rhs_codes, rhs_scales):
+            acc = psum.tile([P, BANK], F32, name="bank", tag="bank")
+            for e in range(PAIR):
+                for g in range(N_PASSES):
+                    cols = slice((e * N_PASSES + g) * P, (e * N_PASSES + g + 1) * P)
+                    nc.tensor.matmul_mx(
+                        out=acc[:, e * C : (e + 1) * C],
+                        lhsT=a_codes[i][b][:, cols].bitcast(FP8X4),
+                        lhsT_scale=a_scales[i][b][:, cols],
+                        rhs=rhs_codes[:, g, :].bitcast(FP8X4),
+                        rhs_scale=rhs_scales[:, g, :],
+                        start=(g == 0),
+                        stop=(g == N_PASSES - 1),
+                    )
+            return acc
+
+        t1_rows = {}
+
+        def first_product(i, b, store_queue):
+            acc = product_with_a(i, b, cand_codes, cand_scales)
+            g, u = divmod(b, GROUPS_PER_PASS)
+            if u == 0:
+                t1_rows[i] = stream.tile([P, PACK, C], F32, name="t1_rows", tag="t1_rows", bufs=3)
+            rows = t1_rows[i][:, u * PAIR : (u + 1) * PAIR, :]
+            nc.scalar.copy(out=rows, in_=acc[:].rearrange("p (e c) -> p e c", e=PAIR))
+            col = (i * TERMS + 1) * C
+            store_queue.dma_start(out=out_groups[b][:, :, col : col + C], in_=rows)
+            if u == GROUPS_PER_PASS - 1:
+                quantise_rows(t1_rows[i][:], t1_codes[i], t1_scales[i], g)
+
+        def second_product(i, b):
+            acc = product_with_a(i, b, t1_codes[i], t1_scales[i])
+            t2_rows = stream.tile([P, PAIR, C], F32, name="t2_rows", tag="t2_rows", bufs=3)
+            nc.vector.scalar_tensor_tensor(
+                out=t2_rows[:].rearrange("p e c -> p (e c)"),
+                in0=acc[:],
+                scalar=2.0,
+                in1=cand[:, b * PAIR : (b + 1) * PAIR, :].rearrange("p e c -> p (e c)"),
+                op0=ALU.mult,
+                op1=ALU.subtract,
+            )
+            col = (i * TERMS + 2) * C
+            nc.sync.dma_start(out=out_groups[b][:, :, col : col + C], in_=t2_rows[:])
+
+        z_t = {}
+        for k in range(N_GROUPS):
+            xg_t = transpose_xg_group(k)
+            transpose_a_group(0, k)
+            if k > 0:
+                finish_cand(k - 1, z_t[k - 1])
+            z_t[k] = gate_matmuls(xg_t)
+        transpose_a_group(1, 0)
+        finish_cand(N_GROUPS - 1, z_t[N_GROUPS - 1])
+        for b in range(N_GROUPS):
+            if b + 1 < N_GROUPS:
+                transpose_a_group(1, b + 1)
+            first_product(0, b, nc.gpsimd)
+        quantise_a_group(SUPPORTS - 1, N_GROUPS - 1)
+        for b in range(N_GROUPS):
+            first_product(1, b, nc.sync)
+        for b in range(N_GROUPS):
+            second_product(0, b)
+        for b in range(N_GROUPS):
+            second_product(1, b)

@@ -27,7 +27,12 @@ D_STATE = 64
 C = D_IN + 2 * D_STATE
 BANK = 512
 PER_BANK = BANK // P
-TERMS = 3
+CAND = 0
+CAND_AGAIN = 3
+T1 = (1, 4)
+T2 = (2, 5)
+N_TERMS = 6
+TERMS_PER_STORE = 2
 
 FLOPS = 2 * NODES * F_GATE * P + 2 * SUPPORTS * 2 * NODES * NODES * C
 
@@ -40,7 +45,7 @@ def tile_dgggl_pa_kernel(tc, xg_gate, gate_w_z, gate_b_z, xt, state1, state2, su
 
     with ExitStack() as ctx:
         keep = ctx.enter_context(tc.tile_pool(name="keep", bufs=1))
-        stream = ctx.enter_context(tc.tile_pool(name="stream", bufs=2))
+        work = ctx.enter_context(tc.tile_pool(name="work", bufs=2))
         psum = ctx.enter_context(tc.psum_pool(name="psum", bufs=8))
         ctx.enter_context(tc.manual_schedule())
 
@@ -49,43 +54,6 @@ def tile_dgggl_pa_kernel(tc, xg_gate, gate_w_z, gate_b_z, xt, state1, state2, su
         table_warmer = keep.tile([P, 1], F32)
         nc.scalar.activation(out=table_warmer[:], in_=ident[:, 0:1], func=ACT.Sigmoid)
 
-        xg_raw = []
-        a_raw = [[], []]
-
-        def load_xg(k):
-            raw = stream.tile([P, PAIR * F_GATE], BF16, name="xg_raw_%d" % k, tag="xg_raw", bufs=3)
-            nc.sync.dma_start(out=raw[:], in_=xg_groups[k])
-            xg_raw.append(raw)
-
-        def load_a(i, b):
-            raw = stream.tile([P, PAIR * NODES], BF16, name="a_raw_%d_%d" % (i, b), tag="a_raw", bufs=4)
-            a_groups = supports[i, 0].rearrange("(g r e) m -> g r (e m)", r=P, e=PAIR)
-            nc.sync.dma_start(out=raw[:], in_=a_groups[b])
-            a_raw[i].append(raw)
-
-        load_xg(0)
-        w_sb = keep.tile([P, F_CHUNKS, PAIR * P], BF16)
-        nc.sync.dma_start(out=w_sb[:], in_=gate_w_z.rearrange("(j q e) c -> q j (e c)", q=P, e=PAIR))
-        bias_bf = keep.tile([P, 1], BF16)
-        with nc.allow_non_contiguous_dma(reason="128 bias values, one to a partition"):
-            nc.sync.dma_start(out=bias_bf[:], in_=gate_b_z.rearrange("(c o) -> c o", o=1))
-        load_a(0, 0)
-        xt_sb = keep.tile([P, N_GROUPS, PAIR * D_IN], BF16)
-        nc.sync.dma_start(out=xt_sb[:], in_=xt[0].rearrange("(g r e) c -> r g (e c)", r=P, e=PAIR))
-        s1_sb = keep.tile([P, N_GROUPS, PAIR * D_STATE], BF16)
-        nc.sync.dma_start(out=s1_sb[:], in_=state1[0].rearrange("(g r e) c -> r g (e c)", r=P, e=PAIR))
-        s2_sb = keep.tile([P, N_GROUPS, PAIR * D_STATE], BF16)
-        nc.sync.dma_start(out=s2_sb[:], in_=state2[0].rearrange("(g r e) c -> r g (e c)", r=P, e=PAIR))
-        for k in range(1, N_GROUPS):
-            load_xg(k)
-            load_a(0, k)
-        for b in range(N_GROUPS):
-            load_a(1, b)
-
-        bias = keep.tile([P, 1], F32)
-        nc.vector.tensor_copy(out=bias[:], in_=bias_bf[:])
-
-        cand = keep.tile([P, N_GROUPS * PAIR, C], F32)
         a_codes = [[], []]
         a_scales = [[], []]
         for i in range(SUPPORTS):
@@ -103,101 +71,25 @@ def tile_dgggl_pa_kernel(tc, xg_gate, gate_w_z, gate_b_z, xt, state1, state2, su
         for i in range(SUPPORTS):
             t1_codes.append(keep.tile([P, N_PASSES, C], U32, name="t1_codes_%d" % i, align_bytes=64))
             t1_scales.append(keep.tile([P, N_PASSES, C], U8, name="t1_scales_%d" % i, align_bytes=64))
+        out_sb = [keep.tile([P, N_GROUPS * PAIR, TERMS_PER_STORE * C], F32, name="out_sb_0")]
 
-        def empty_bank(position, run, dst, src):
-            if position == run - 1:
-                nc.vector.tensor_copy(out=dst, in_=src)
-            else:
-                nc.scalar.copy(out=dst, in_=src)
+        def term(which, first_block, n_blocks):
+            h, half = divmod(which, TERMS_PER_STORE)
+            return out_sb[h][:, first_block : first_block + n_blocks, half * C : (half + 1) * C]
 
-        def transpose_xg_group(k):
-            words = xg_raw[k][:].bitcast(F32)
-            xg_t = stream.tile([P, F_CHUNKS * GROUP], F32, name="xg_t", tag="xg_t")
-            n_banks = F_CHUNKS * PAIR // PER_BANK
-            for bank_no in range(n_banks):
-                bank = psum.tile([P, BANK], F32, name="bank", tag="bank")
-                for s in range(PER_BANK):
-                    j, e = divmod(bank_no * PER_BANK + s, PAIR)
-                    col = (e * F_CHUNKS + j) * P
-                    nc.tensor.transpose(bank[:, s * P : (s + 1) * P], words[:, col : col + P], ident[:])
-                empty_bank(bank_no, n_banks, xg_t[:, bank_no * BANK : (bank_no + 1) * BANK], bank[:])
-            return xg_t
+        def store(h, b):
+            width = TERMS_PER_STORE * C
+            nc.sync.dma_start(
+                out=out_groups[b][:, :, h * width : (h + 1) * width], in_=out_sb[h][:, b * PAIR : (b + 1) * PAIR, :]
+            )
 
-        def gate_matmuls(xg_t):
-            halves = xg_t[:].bitcast(BF16).rearrange("p (j n e) -> p j n e", j=F_CHUNKS, e=PAIR)
-            acc = psum.tile([P, BANK], F32, name="bank", tag="bank")
-            for j in range(F_CHUNKS):
-                for e in range(PAIR):
-                    nc.tensor.matmul(
-                        out=acc[:, 0:GROUP],
-                        lhsT=w_sb[:, j, e * P : (e + 1) * P],
-                        rhs=halves[:, j, :, e],
-                        start=(j == 0 and e == 0),
-                        stop=(j == F_CHUNKS - 1 and e == PAIR - 1),
-                    )
-            z_t = stream.tile([P, GROUP], F32, name="z_t", tag="z_t")
-            nc.scalar.activation(out=z_t[:], in_=acc[:, 0:GROUP], func=ACT.Sigmoid, bias=bias[:, 0:1], scale=1.0)
-            return z_t
-
-        def quantise_rows(rows, codes, scales, g):
-            grouped = stream.tile([P, C * PACK], BF16, name="rows_grouped", tag="rows_grouped", align_bytes=64)
+        def quantise_rows(which, g, codes, scales):
+            grouped = work.tile([P, C * PACK], BF16, name="rows_grouped", tag="rows_grouped", align_bytes=64)
             nc.vector.tensor_copy(
-                out=grouped[:].rearrange("p (c t) -> p c t", t=PACK), in_=rows.rearrange("p t c -> p c t")
+                out=grouped[:].rearrange("p (c t) -> p c t", t=PACK),
+                in_=term(which, g * PACK, PACK).rearrange("p t c -> p c t"),
             )
             nc.vector.quantize_mx(out=codes[:, g, :].bitcast(FP8X4), scales=scales[:, g, :], in_=grouped[:])
-
-        def finish_cand(k, z_t):
-            bank = psum.tile([P, BANK], F32, name="bank", tag="bank")
-            for e in range(PAIR):
-                nc.tensor.transpose(bank[:, e * P : (e + 1) * P], z_t[:, e * P : (e + 1) * P], ident[:])
-            z = bank[:, 0:GROUP].rearrange("p (e c) -> p e c", e=PAIR)
-            rows = cand[:, k * PAIR : (k + 1) * PAIR, :]
-            nc.scalar.copy(out=rows[:, :, 0:D_IN], in_=xt_sb[:, k, :].rearrange("p (e c) -> p e c", e=PAIR))
-            nc.vector.tensor_tensor(
-                out=rows[:, :, D_IN : D_IN + D_STATE],
-                in0=z[:, :, 0:D_STATE],
-                in1=s1_sb[:, k, :].rearrange("p (e c) -> p e c", e=PAIR),
-                op=ALU.mult,
-            )
-            nc.vector.tensor_tensor(
-                out=rows[:, :, D_IN + D_STATE : C],
-                in0=z[:, :, D_STATE : 2 * D_STATE],
-                in1=s2_sb[:, k, :].rearrange("p (e c) -> p e c", e=PAIR),
-                op=ALU.mult,
-            )
-            for i in range(SUPPORTS):
-                nc.gpsimd.dma_start(out=out_groups[k][:, :, i * TERMS * C : i * TERMS * C + C], in_=rows)
-            g, u = divmod(k, GROUPS_PER_PASS)
-            if u == GROUPS_PER_PASS - 1:
-                quantise_rows(cand[:, g * PACK : (g + 1) * PACK, :], cand_codes, cand_scales, g)
-
-        a_grouped = {}
-
-        def quantise_a_group(i, b):
-            nc.vector.quantize_mx(
-                out=a_codes[i][b][:].bitcast(FP8X4), scales=a_scales[i][b][:], in_=a_grouped[(i, b)][:]
-            )
-
-        def transpose_a_group(i, b):
-            words = a_raw[i][b][:].bitcast(F32)
-            grouped = stream.tile([P, PAIR * NODES], BF16, name="a_grouped", tag="a_grouped", align_bytes=64)
-            grouped_words = grouped[:].bitcast(F32).rearrange("p (x r u) -> p x r u", r=P, u=PAIR)
-            n_banks = NODES // BANK
-            for bank_no in range(n_banks):
-                bank = psum.tile([P, BANK], F32, name="bank", tag="bank")
-                for s in range(PER_BANK):
-                    col = (bank_no * PER_BANK + s) * P
-                    nc.tensor.transpose(bank[:, s * P : (s + 1) * P], words[:, col : col + P], ident[:])
-                empty_bank(
-                    bank_no,
-                    n_banks,
-                    grouped_words[:, bank_no * PAIR : (bank_no + 1) * PAIR, :, :],
-                    bank[:].rearrange("p (x u r) -> p x r u", u=PAIR, r=P),
-                )
-            a_grouped[(i, b)] = grouped
-            if (i, b) != (0, 0):
-                before_i, before_b = divmod(i * N_GROUPS + b - 1, N_GROUPS)
-                quantise_a_group(before_i, before_b)
 
         def product_with_a(i, b, rhs_codes, rhs_scales):
             acc = psum.tile([P, BANK], F32, name="bank", tag="bank")
@@ -213,53 +105,178 @@ def tile_dgggl_pa_kernel(tc, xg_gate, gate_w_z, gate_b_z, xt, state1, state2, su
                         start=(g == 0),
                         stop=(g == N_PASSES - 1),
                     )
-            return acc
+            return acc[:].rearrange("p (e c) -> p e c", e=PAIR)
 
-        t1_rows = {}
-
-        def first_product(i, b, store_queue):
+        def first_product(i, b):
             acc = product_with_a(i, b, cand_codes, cand_scales)
+            nc.scalar.copy(out=term(T1[i], b * PAIR, PAIR), in_=acc)
             g, u = divmod(b, GROUPS_PER_PASS)
-            if u == 0:
-                t1_rows[i] = stream.tile([P, PACK, C], F32, name="t1_rows", tag="t1_rows", bufs=3)
-            rows = t1_rows[i][:, u * PAIR : (u + 1) * PAIR, :]
-            nc.scalar.copy(out=rows, in_=acc[:].rearrange("p (e c) -> p e c", e=PAIR))
-            col = (i * TERMS + 1) * C
-            store_queue.dma_start(out=out_groups[b][:, :, col : col + C], in_=rows)
             if u == GROUPS_PER_PASS - 1:
-                quantise_rows(t1_rows[i][:], t1_codes[i], t1_scales[i], g)
+                quantise_rows(T1[i], g, t1_codes[i], t1_scales[i])
 
         def second_product(i, b):
             acc = product_with_a(i, b, t1_codes[i], t1_scales[i])
-            t2_rows = stream.tile([P, PAIR, C], F32, name="t2_rows", tag="t2_rows", bufs=3)
             nc.vector.scalar_tensor_tensor(
-                out=t2_rows[:].rearrange("p e c -> p (e c)"),
-                in0=acc[:],
+                out=term(T2[i], b * PAIR, PAIR),
+                in0=acc,
                 scalar=2.0,
-                in1=cand[:, b * PAIR : (b + 1) * PAIR, :].rearrange("p e c -> p (e c)"),
+                in1=term(CAND, b * PAIR, PAIR),
                 op0=ALU.mult,
                 op1=ALU.subtract,
             )
-            col = (i * TERMS + 2) * C
-            nc.sync.dma_start(out=out_groups[b][:, :, col : col + C], in_=t2_rows[:])
 
-        z_t = {}
-        for k in range(N_GROUPS):
-            xg_t = transpose_xg_group(k)
-            transpose_a_group(0, k)
-            if k > 0:
-                finish_cand(k - 1, z_t[k - 1])
-            z_t[k] = gate_matmuls(xg_t)
-        transpose_a_group(1, 0)
-        finish_cand(N_GROUPS - 1, z_t[N_GROUPS - 1])
-        for b in range(N_GROUPS):
-            if b + 1 < N_GROUPS:
-                transpose_a_group(1, b + 1)
-            first_product(0, b, nc.gpsimd)
-        quantise_a_group(SUPPORTS - 1, N_GROUPS - 1)
-        for b in range(N_GROUPS):
-            first_product(1, b, nc.sync)
-        for b in range(N_GROUPS):
-            second_product(0, b)
-        for b in range(N_GROUPS):
-            second_product(1, b)
+        with tc.tile_pool(name="stream", bufs=2) as stream:
+            xg_raw = []
+            a_raw = [[], []]
+
+            def load_xg(k):
+                raw = stream.tile([P, PAIR * F_GATE], BF16, name="xg_raw_%d" % k, tag="xg_raw", bufs=3)
+                nc.sync.dma_start(out=raw[:], in_=xg_groups[k])
+                xg_raw.append(raw)
+
+            def load_a(i, b):
+                raw = stream.tile([P, PAIR * NODES], BF16, name="a_raw_%d_%d" % (i, b), tag="a_raw", bufs=4)
+                a_groups = supports[i, 0].rearrange("(g r e) m -> g r (e m)", r=P, e=PAIR)
+                nc.sync.dma_start(out=raw[:], in_=a_groups[b])
+                a_raw[i].append(raw)
+
+            load_xg(0)
+            w_sb = keep.tile([P, F_CHUNKS, PAIR * P], BF16)
+            nc.sync.dma_start(out=w_sb[:], in_=gate_w_z.rearrange("(j q e) c -> q j (e c)", q=P, e=PAIR))
+            bias_bf = keep.tile([P, 1], BF16)
+            with nc.allow_non_contiguous_dma(reason="128 bias values, one to a partition"):
+                nc.sync.dma_start(out=bias_bf[:], in_=gate_b_z.rearrange("(c o) -> c o", o=1))
+            load_a(0, 0)
+            xt_sb = keep.tile([P, N_GROUPS, PAIR * D_IN], BF16)
+            nc.sync.dma_start(out=xt_sb[:], in_=xt[0].rearrange("(g r e) c -> r g (e c)", r=P, e=PAIR))
+            s1_sb = keep.tile([P, N_GROUPS, PAIR * D_STATE], BF16)
+            nc.sync.dma_start(out=s1_sb[:], in_=state1[0].rearrange("(g r e) c -> r g (e c)", r=P, e=PAIR))
+            s2_sb = keep.tile([P, N_GROUPS, PAIR * D_STATE], BF16)
+            nc.sync.dma_start(out=s2_sb[:], in_=state2[0].rearrange("(g r e) c -> r g (e c)", r=P, e=PAIR))
+            for k in range(1, N_GROUPS):
+                load_xg(k)
+                load_a(0, k)
+            for b in range(N_GROUPS):
+                load_a(1, b)
+
+            bias = keep.tile([P, 1], F32)
+            nc.vector.tensor_copy(out=bias[:], in_=bias_bf[:])
+
+            def empty_bank(position, run, dst, src):
+                if position == run - 1:
+                    nc.vector.tensor_copy(out=dst, in_=src)
+                else:
+                    nc.scalar.copy(out=dst, in_=src)
+
+            def transpose_xg_group(k):
+                words = xg_raw[k][:].bitcast(F32)
+                xg_t = stream.tile([P, F_CHUNKS * GROUP], F32, name="xg_t", tag="xg_t")
+                n_banks = F_CHUNKS * PAIR // PER_BANK
+                for bank_no in range(n_banks):
+                    bank = psum.tile([P, BANK], F32, name="bank", tag="bank")
+                    for s in range(PER_BANK):
+                        j, e = divmod(bank_no * PER_BANK + s, PAIR)
+                        col = (e * F_CHUNKS + j) * P
+                        nc.tensor.transpose(bank[:, s * P : (s + 1) * P], words[:, col : col + P], ident[:])
+                    empty_bank(bank_no, n_banks, xg_t[:, bank_no * BANK : (bank_no + 1) * BANK], bank[:])
+                return xg_t
+
+            def gate_matmuls(xg_t):
+                halves = xg_t[:].bitcast(BF16).rearrange("p (j n e) -> p j n e", j=F_CHUNKS, e=PAIR)
+                acc = psum.tile([P, BANK], F32, name="bank", tag="bank")
+                for j in range(F_CHUNKS):
+                    for e in range(PAIR):
+                        nc.tensor.matmul(
+                            out=acc[:, 0:GROUP],
+                            lhsT=w_sb[:, j, e * P : (e + 1) * P],
+                            rhs=halves[:, j, :, e],
+                            start=(j == 0 and e == 0),
+                            stop=(j == F_CHUNKS - 1 and e == PAIR - 1),
+                        )
+                z_t = stream.tile([P, GROUP], F32, name="z_t", tag="z_t")
+                nc.scalar.activation(
+                    out=z_t[:], in_=acc[:, 0:GROUP], func=ACT.Sigmoid, bias=bias[:, 0:1], scale=1.0
+                )
+                return z_t
+
+            def finish_cand(k, z_t):
+                bank = psum.tile([P, BANK], F32, name="bank", tag="bank")
+                for e in range(PAIR):
+                    nc.tensor.transpose(bank[:, e * P : (e + 1) * P], z_t[:, e * P : (e + 1) * P], ident[:])
+                z = bank[:, 0:GROUP].rearrange("p (e c) -> p e c", e=PAIR)
+                rows = term(CAND, k * PAIR, PAIR)
+                nc.scalar.copy(out=rows[:, :, 0:D_IN], in_=xt_sb[:, k, :].rearrange("p (e c) -> p e c", e=PAIR))
+                nc.vector.tensor_tensor(
+                    out=rows[:, :, D_IN : D_IN + D_STATE],
+                    in0=z[:, :, 0:D_STATE],
+                    in1=s1_sb[:, k, :].rearrange("p (e c) -> p e c", e=PAIR),
+                    op=ALU.mult,
+                )
+                nc.vector.tensor_tensor(
+                    out=rows[:, :, D_IN + D_STATE : C],
+                    in0=z[:, :, D_STATE : 2 * D_STATE],
+                    in1=s2_sb[:, k, :].rearrange("p (e c) -> p e c", e=PAIR),
+                    op=ALU.mult,
+                )
+                g, u = divmod(k, GROUPS_PER_PASS)
+                if u == GROUPS_PER_PASS - 1:
+                    quantise_rows(CAND, g, cand_codes, cand_scales)
+
+            a_grouped = {}
+
+            def quantise_a_group(i, b):
+                nc.vector.quantize_mx(
+                    out=a_codes[i][b][:].bitcast(FP8X4), scales=a_scales[i][b][:], in_=a_grouped[(i, b)][:]
+                )
+
+            def transpose_a_group(i, b):
+                words = a_raw[i][b][:].bitcast(F32)
+                grouped = stream.tile(
+                    [P, PAIR * NODES], BF16, name="a_grouped", tag="a_grouped", bufs=3, align_bytes=64
+                )
+                grouped_words = grouped[:].bitcast(F32).rearrange("p (x r u) -> p x r u", r=P, u=PAIR)
+                n_banks = NODES // BANK
+                for bank_no in range(n_banks):
+                    bank = psum.tile([P, BANK], F32, name="bank", tag="bank")
+                    for s in range(PER_BANK):
+                        col = (bank_no * PER_BANK + s) * P
+                        nc.tensor.transpose(bank[:, s * P : (s + 1) * P], words[:, col : col + P], ident[:])
+                    empty_bank(
+                        bank_no,
+                        n_banks,
+                        grouped_words[:, bank_no * PAIR : (bank_no + 1) * PAIR, :, :],
+                        bank[:].rearrange("p (x u r) -> p x r u", u=PAIR, r=P),
+                    )
+                a_grouped[(i, b)] = grouped
+                if (i, b) != (0, 0):
+                    before_i, before_b = divmod(i * N_GROUPS + b - 1, N_GROUPS)
+                    quantise_a_group(before_i, before_b)
+
+            z_t = {}
+            for k in range(N_GROUPS):
+                xg_t = transpose_xg_group(k)
+                transpose_a_group(0, k)
+                if k > 0:
+                    finish_cand(k - 1, z_t[k - 1])
+                z_t[k] = gate_matmuls(xg_t)
+            transpose_a_group(1, 0)
+            finish_cand(N_GROUPS - 1, z_t[N_GROUPS - 1])
+            for b in range(N_GROUPS):
+                if b + 1 < N_GROUPS:
+                    transpose_a_group(1, b + 1)
+                first_product(0, b)
+                store(T1[0] // TERMS_PER_STORE, b)
+            quantise_a_group(SUPPORTS - 1, N_GROUPS - 1)
+
+        with tc.tile_pool(name="late", bufs=1) as late:
+            for h in range(1, N_TERMS // TERMS_PER_STORE):
+                out_sb.append(late.tile([P, N_GROUPS * PAIR, TERMS_PER_STORE * C], F32, name="out_sb_%d" % h))
+            for b in range(N_GROUPS):
+                first_product(1, b)
+                nc.scalar.copy(out=term(CAND_AGAIN, b * PAIR, PAIR), in_=term(CAND, b * PAIR, PAIR))
+            for b in range(N_GROUPS):
+                second_product(0, b)
+                store(T2[0] // TERMS_PER_STORE, b)
+            for b in range(N_GROUPS):
+                second_product(1, b)
+                store(T2[1] // TERMS_PER_STORE, b)

@@ -27,12 +27,12 @@ D_STATE = 64
 C = D_IN + 2 * D_STATE
 BANK = 512
 PER_BANK = BANK // P
+A_BANKS = NODES // BANK
 CAND = 0
 CAND_AGAIN = 3
 T1 = (1, 4)
 T2 = (2, 5)
-N_TERMS = 6
-TERMS_PER_STORE = 2
+STORES = ((CAND, T1[0]), (T2[0], CAND_AGAIN), (T1[1],), (T2[1],))
 
 FLOPS = 2 * NODES * F_GATE * P + 2 * SUPPORTS * 2 * NODES * NODES * C
 
@@ -71,16 +71,19 @@ def tile_dgggl_pa_kernel(tc, xg_gate, gate_w_z, gate_b_z, xt, state1, state2, su
         for i in range(SUPPORTS):
             t1_codes.append(keep.tile([P, N_PASSES, C], U32, name="t1_codes_%d" % i, align_bytes=64))
             t1_scales.append(keep.tile([P, N_PASSES, C], U8, name="t1_scales_%d" % i, align_bytes=64))
-        out_sb = [keep.tile([P, N_GROUPS * PAIR, TERMS_PER_STORE * C], F32, name="out_sb_0")]
+        out_sb = [keep.tile([P, N_GROUPS * PAIR, len(STORES[0]) * C], F32, name="out_sb_0")]
 
         def term(which, first_block, n_blocks):
-            h, half = divmod(which, TERMS_PER_STORE)
-            return out_sb[h][:, first_block : first_block + n_blocks, half * C : (half + 1) * C]
+            h = [which in terms for terms in STORES].index(True)
+            col = STORES[h].index(which) * C
+            return out_sb[h][:, first_block : first_block + n_blocks, col : col + C]
 
-        def store(h, b):
-            width = TERMS_PER_STORE * C
+        def store(which, b):
+            h = [which in terms for terms in STORES].index(True)
+            col = STORES[h][0] * C
             nc.sync.dma_start(
-                out=out_groups[b][:, :, h * width : (h + 1) * width], in_=out_sb[h][:, b * PAIR : (b + 1) * PAIR, :]
+                out=out_groups[b][:, :, col : col + len(STORES[h]) * C],
+                in_=out_sb[h][:, b * PAIR : (b + 1) * PAIR, :],
             )
 
         def quantise_rows(which, g, codes, scales):
@@ -146,6 +149,7 @@ def tile_dgggl_pa_kernel(tc, xg_gate, gate_w_z, gate_b_z, xt, state1, state2, su
             bias_bf = keep.tile([P, 1], BF16)
             with nc.allow_non_contiguous_dma(reason="128 bias values, one to a partition"):
                 nc.sync.dma_start(out=bias_bf[:], in_=gate_b_z.rearrange("(c o) -> c o", o=1))
+            load_xg(1)
             load_a(0, 0)
             xt_sb = keep.tile([P, N_GROUPS, PAIR * D_IN], BF16)
             nc.sync.dma_start(out=xt_sb[:], in_=xt[0].rearrange("(g r e) c -> r g (e c)", r=P, e=PAIR))
@@ -153,9 +157,10 @@ def tile_dgggl_pa_kernel(tc, xg_gate, gate_w_z, gate_b_z, xt, state1, state2, su
             nc.sync.dma_start(out=s1_sb[:], in_=state1[0].rearrange("(g r e) c -> r g (e c)", r=P, e=PAIR))
             s2_sb = keep.tile([P, N_GROUPS, PAIR * D_STATE], BF16)
             nc.sync.dma_start(out=s2_sb[:], in_=state2[0].rearrange("(g r e) c -> r g (e c)", r=P, e=PAIR))
-            for k in range(1, N_GROUPS):
+            for k in range(2, N_GROUPS):
                 load_xg(k)
-                load_a(0, k)
+                load_a(0, k - 1)
+            load_a(0, N_GROUPS - 1)
             for b in range(N_GROUPS):
                 load_a(1, b)
 
@@ -181,18 +186,20 @@ def tile_dgggl_pa_kernel(tc, xg_gate, gate_w_z, gate_b_z, xt, state1, state2, su
                     empty_bank(bank_no, n_banks, xg_t[:, bank_no * BANK : (bank_no + 1) * BANK], bank[:])
                 return xg_t
 
-            def gate_matmuls(xg_t):
+            def gate_matmuls(acc, xg_t, quarter):
                 halves = xg_t[:].bitcast(BF16).rearrange("p (j n e) -> p j n e", j=F_CHUNKS, e=PAIR)
-                acc = psum.tile([P, BANK], F32, name="bank", tag="bank")
-                for j in range(F_CHUNKS):
-                    for e in range(PAIR):
-                        nc.tensor.matmul(
-                            out=acc[:, 0:GROUP],
-                            lhsT=w_sb[:, j, e * P : (e + 1) * P],
-                            rhs=halves[:, j, :, e],
-                            start=(j == 0 and e == 0),
-                            stop=(j == F_CHUNKS - 1 and e == PAIR - 1),
-                        )
+                n_matmuls = F_CHUNKS * PAIR
+                for n in range(quarter * n_matmuls // A_BANKS, (quarter + 1) * n_matmuls // A_BANKS):
+                    j, e = divmod(n, PAIR)
+                    nc.tensor.matmul(
+                        out=acc[:, 0:GROUP],
+                        lhsT=w_sb[:, j, e * P : (e + 1) * P],
+                        rhs=halves[:, j, :, e],
+                        start=(n == 0),
+                        stop=(n == n_matmuls - 1),
+                    )
+
+            def sigmoid(acc):
                 z_t = stream.tile([P, GROUP], F32, name="z_t", tag="z_t")
                 nc.scalar.activation(
                     out=z_t[:], in_=acc[:, 0:GROUP], func=ACT.Sigmoid, bias=bias[:, 0:1], scale=1.0
@@ -229,54 +236,63 @@ def tile_dgggl_pa_kernel(tc, xg_gate, gate_w_z, gate_b_z, xt, state1, state2, su
                     out=a_codes[i][b][:].bitcast(FP8X4), scales=a_scales[i][b][:], in_=a_grouped[(i, b)][:]
                 )
 
-            def transpose_a_group(i, b):
-                words = a_raw[i][b][:].bitcast(F32)
-                grouped = stream.tile(
-                    [P, PAIR * NODES], BF16, name="a_grouped", tag="a_grouped", bufs=3, align_bytes=64
-                )
-                grouped_words = grouped[:].bitcast(F32).rearrange("p (x r u) -> p x r u", r=P, u=PAIR)
-                n_banks = NODES // BANK
-                for bank_no in range(n_banks):
-                    bank = psum.tile([P, BANK], F32, name="bank", tag="bank")
-                    for s in range(PER_BANK):
-                        col = (bank_no * PER_BANK + s) * P
-                        nc.tensor.transpose(bank[:, s * P : (s + 1) * P], words[:, col : col + P], ident[:])
-                    empty_bank(
-                        bank_no,
-                        n_banks,
-                        grouped_words[:, bank_no * PAIR : (bank_no + 1) * PAIR, :, :],
-                        bank[:].rearrange("p (x u r) -> p x r u", u=PAIR, r=P),
+            def transpose_a_bank(i, b, bank_no):
+                if bank_no == 0:
+                    a_grouped[(i, b)] = stream.tile(
+                        [P, PAIR * NODES], BF16, name="a_grouped", tag="a_grouped", bufs=3, align_bytes=64
                     )
-                a_grouped[(i, b)] = grouped
-                if (i, b) != (0, 0):
-                    before_i, before_b = divmod(i * N_GROUPS + b - 1, N_GROUPS)
-                    quantise_a_group(before_i, before_b)
+                words = a_raw[i][b][:].bitcast(F32)
+                grouped_words = a_grouped[(i, b)][:].bitcast(F32).rearrange("p (x r u) -> p x r u", r=P, u=PAIR)
+                bank = psum.tile([P, BANK], F32, name="bank", tag="bank")
+                for s in range(PER_BANK):
+                    col = (bank_no * PER_BANK + s) * P
+                    nc.tensor.transpose(bank[:, s * P : (s + 1) * P], words[:, col : col + P], ident[:])
+                empty_bank(
+                    bank_no,
+                    A_BANKS,
+                    grouped_words[:, bank_no * PAIR : (bank_no + 1) * PAIR, :, :],
+                    bank[:].rearrange("p (x u r) -> p x r u", u=PAIR, r=P),
+                )
+                if bank_no == A_BANKS - 1 and (i, b) != (0, 0):
+                    quantise_a_group(*divmod(i * N_GROUPS + b - 1, N_GROUPS))
+
+            def transpose_a_group(i, b):
+                for bank_no in range(A_BANKS):
+                    transpose_a_bank(i, b, bank_no)
 
             z_t = {}
-            for k in range(N_GROUPS):
-                xg_t = transpose_xg_group(k)
-                transpose_a_group(0, k)
+            for k in range(N_GROUPS + 1):
+                if k < N_GROUPS:
+                    xg_t = transpose_xg_group(k)
                 if k > 0:
                     finish_cand(k - 1, z_t[k - 1])
-                z_t[k] = gate_matmuls(xg_t)
+                if k < N_GROUPS:
+                    gate_acc = psum.tile([P, BANK], F32, name="bank", tag="bank")
+                for quarter in range(A_BANKS):
+                    if k > 0:
+                        transpose_a_bank(0, k - 1, quarter)
+                    if k < N_GROUPS:
+                        gate_matmuls(gate_acc, xg_t, quarter)
+                if k < N_GROUPS:
+                    z_t[k] = sigmoid(gate_acc)
             transpose_a_group(1, 0)
-            finish_cand(N_GROUPS - 1, z_t[N_GROUPS - 1])
             for b in range(N_GROUPS):
                 if b + 1 < N_GROUPS:
                     transpose_a_group(1, b + 1)
                 first_product(0, b)
-                store(T1[0] // TERMS_PER_STORE, b)
+                store(T1[0], b)
             quantise_a_group(SUPPORTS - 1, N_GROUPS - 1)
 
         with tc.tile_pool(name="late", bufs=1) as late:
-            for h in range(1, N_TERMS // TERMS_PER_STORE):
-                out_sb.append(late.tile([P, N_GROUPS * PAIR, TERMS_PER_STORE * C], F32, name="out_sb_%d" % h))
+            for h in range(1, len(STORES)):
+                out_sb.append(late.tile([P, N_GROUPS * PAIR, len(STORES[h]) * C], F32, name="out_sb_%d" % h))
             for b in range(N_GROUPS):
                 first_product(1, b)
+                store(T1[1], b)
                 nc.scalar.copy(out=term(CAND_AGAIN, b * PAIR, PAIR), in_=term(CAND, b * PAIR, PAIR))
             for b in range(N_GROUPS):
                 second_product(0, b)
-                store(T2[0] // TERMS_PER_STORE, b)
+                store(T2[0], b)
             for b in range(N_GROUPS):
                 second_product(1, b)
-                store(T2[1] // TERMS_PER_STORE, b)
+                store(T2[1], b)

@@ -32,7 +32,8 @@ CAND = 0
 CAND_AGAIN = 3
 T1 = (1, 4)
 T2 = (2, 5)
-STORES = ((CAND, T1[0]), (T2[0], CAND_AGAIN), (T1[1],), (T2[1],))
+
+RAW_BUFS = 6
 
 FLOPS = 2 * NODES * F_GATE * P + 2 * SUPPORTS * 2 * NODES * NODES * C
 
@@ -41,6 +42,7 @@ def tile_dgggl_pa_kernel(tc, xg_gate, gate_w_z, gate_b_z, xt, state1, state2, su
     nc = tc.nc
 
     xg_groups = xg_gate[0].rearrange("(g r e) f -> g r (e f)", r=P, e=PAIR)
+    a_groups = [supports[i, 0].rearrange("(g r e) m -> g r (e m)", r=P, e=PAIR) for i in range(SUPPORTS)]
     out_groups = out[0].rearrange("(g r e) f -> g r e f", r=P, e=PAIR)
 
     with ExitStack() as ctx:
@@ -54,16 +56,6 @@ def tile_dgggl_pa_kernel(tc, xg_gate, gate_w_z, gate_b_z, xt, state1, state2, su
         table_warmer = keep.tile([P, 1], F32)
         nc.scalar.activation(out=table_warmer[:], in_=ident[:, 0:1], func=ACT.Sigmoid)
 
-        a_codes = [[], []]
-        a_scales = [[], []]
-        for i in range(SUPPORTS):
-            for b in range(N_GROUPS):
-                a_codes[i].append(
-                    keep.tile([P, PAIR * N_PASSES * P], U32, name="a_codes_%d_%d" % (i, b), align_bytes=64)
-                )
-                a_scales[i].append(
-                    keep.tile([P, PAIR * N_PASSES * P], U8, name="a_scales_%d_%d" % (i, b), align_bytes=64)
-                )
         cand_codes = keep.tile([P, N_PASSES, C], U32, align_bytes=64)
         cand_scales = keep.tile([P, N_PASSES, C], U8, align_bytes=64)
         t1_codes = []
@@ -71,38 +63,151 @@ def tile_dgggl_pa_kernel(tc, xg_gate, gate_w_z, gate_b_z, xt, state1, state2, su
         for i in range(SUPPORTS):
             t1_codes.append(keep.tile([P, N_PASSES, C], U32, name="t1_codes_%d" % i, align_bytes=64))
             t1_scales.append(keep.tile([P, N_PASSES, C], U8, name="t1_scales_%d" % i, align_bytes=64))
-        out_sb = [keep.tile([P, N_GROUPS * PAIR, len(STORES[0]) * C], F32, name="out_sb_0")]
+        cand_t1 = keep.tile([P, N_GROUPS * PAIR, 2 * C], F32)
+        t1_last = keep.tile([P, N_GROUPS * PAIR, C], F32)
 
-        def term(which, first_block, n_blocks):
-            h = [which in terms for terms in STORES].index(True)
-            col = STORES[h].index(which) * C
-            return out_sb[h][:, first_block : first_block + n_blocks, col : col + C]
+        def cand_rows(first_block, n_blocks):
+            return cand_t1[:, first_block : first_block + n_blocks, 0:C]
 
-        def store(which, b):
-            h = [which in terms for terms in STORES].index(True)
-            col = STORES[h][0] * C
-            nc.sync.dma_start(
-                out=out_groups[b][:, :, col : col + len(STORES[h]) * C],
-                in_=out_sb[h][:, b * PAIR : (b + 1) * PAIR, :],
+        def t1_rows(i, first_block, n_blocks):
+            if i == 0:
+                return cand_t1[:, first_block : first_block + n_blocks, C : 2 * C]
+            return t1_last[:, first_block : first_block + n_blocks, :]
+
+        def store(first_term, b, rows):
+            col = first_term * C
+            nc.sync.dma_start(out=out_groups[b][:, :, col : col + rows.shape[2]], in_=rows)
+
+        raw = []
+
+        def load(n):
+            kind, b = divmod(n, N_GROUPS)
+            width = PAIR * (F_GATE if kind == 0 else NODES)
+            tile_n = work.tile([P, width], BF16, name="raw_%d" % n, tag="raw", bufs=RAW_BUFS, align_bytes=64)
+            nc.sync.dma_start(out=tile_n[:], in_=xg_groups[b] if kind == 0 else a_groups[kind - 1][b])
+            raw.append(tile_n)
+
+        load(0)
+        w_sb = keep.tile([P, F_CHUNKS, PAIR * P], BF16)
+        nc.sync.dma_start(out=w_sb[:], in_=gate_w_z.rearrange("(j q e) c -> q j (e c)", q=P, e=PAIR))
+        bias_bf = keep.tile([P, 1], BF16)
+        with nc.allow_non_contiguous_dma(reason="128 bias values, one to a partition"):
+            nc.sync.dma_start(out=bias_bf[:], in_=gate_b_z.rearrange("(c o) -> c o", o=1))
+        load(1)
+        xt_sb = keep.tile([P, N_GROUPS, PAIR * D_IN], BF16)
+        nc.sync.dma_start(out=xt_sb[:], in_=xt[0].rearrange("(g r e) c -> r g (e c)", r=P, e=PAIR))
+        s1_sb = keep.tile([P, N_GROUPS, PAIR * D_STATE], BF16)
+        nc.sync.dma_start(out=s1_sb[:], in_=state1[0].rearrange("(g r e) c -> r g (e c)", r=P, e=PAIR))
+        s2_sb = keep.tile([P, N_GROUPS, PAIR * D_STATE], BF16)
+        nc.sync.dma_start(out=s2_sb[:], in_=state2[0].rearrange("(g r e) c -> r g (e c)", r=P, e=PAIR))
+        for n in range(2, RAW_BUFS):
+            load(n)
+
+        bias = keep.tile([P, 1], F32)
+        nc.vector.tensor_copy(out=bias[:], in_=bias_bf[:])
+
+        def new_bank():
+            return psum.tile([P, BANK], F32, name="bank", tag="bank")
+
+        def empty_bank(position, dst, src):
+            if position == 0:
+                nc.vector.tensor_copy(out=dst, in_=src)
+            else:
+                nc.scalar.copy(out=dst, in_=src)
+
+        def transpose_xg_group(k):
+            words = raw[k][:].bitcast(F32)
+            xg_t = work.tile([P, F_CHUNKS * GROUP], F32, name="xg_t", tag="turned", bufs=3, align_bytes=64)
+            for bank_no in range(F_CHUNKS * PAIR // PER_BANK):
+                bank = new_bank()
+                for s in range(PER_BANK):
+                    j, e = divmod(bank_no * PER_BANK + s, PAIR)
+                    col = (e * F_CHUNKS + j) * P
+                    nc.tensor.transpose(bank[:, s * P : (s + 1) * P], words[:, col : col + P], ident[:])
+                empty_bank(bank_no, xg_t[:, bank_no * BANK : (bank_no + 1) * BANK], bank[:])
+            return xg_t
+
+        def transpose_a_group(n):
+            words = raw[n][:].bitcast(F32)
+            a_t = work.tile([P, PAIR * NODES], BF16, name="a_t", tag="turned", bufs=3, align_bytes=64)
+            a_t_words = a_t[:].bitcast(F32).rearrange("p (x r u) -> p x r u", r=P, u=PAIR)
+            for bank_no in range(A_BANKS):
+                bank = new_bank()
+                for s in range(PER_BANK):
+                    col = (bank_no * PER_BANK + s) * P
+                    nc.tensor.transpose(bank[:, s * P : (s + 1) * P], words[:, col : col + P], ident[:])
+                empty_bank(
+                    bank_no,
+                    a_t_words[:, bank_no * PAIR : (bank_no + 1) * PAIR, :, :],
+                    bank[:].rearrange("p (x u r) -> p x r u", u=PAIR, r=P),
+                )
+            return a_t
+
+        def gate(xg_t):
+            acc = new_bank()
+            halves = xg_t[:].bitcast(BF16).rearrange("p (j n e) -> p j n e", j=F_CHUNKS, e=PAIR)
+            for j in range(F_CHUNKS):
+                for e in range(PAIR):
+                    nc.tensor.matmul(
+                        out=acc[:, 0:GROUP],
+                        lhsT=w_sb[:, j, e * P : (e + 1) * P],
+                        rhs=halves[:, j, :, e],
+                        start=(j == 0 and e == 0),
+                        stop=(j == F_CHUNKS - 1 and e == PAIR - 1),
+                    )
+            z_t = work.tile([P, GROUP], F32, name="z_t", tag="z_t")
+            nc.scalar.activation(out=z_t[:], in_=acc[:, 0:GROUP], func=ACT.Sigmoid, bias=bias[:, 0:1], scale=1.0)
+            return z_t
+
+        def turn_z(z_t):
+            bank = new_bank()
+            for e in range(PAIR):
+                nc.tensor.transpose(bank[:, e * P : (e + 1) * P], z_t[:, e * P : (e + 1) * P], ident[:])
+            return bank[:, 0:GROUP].rearrange("p (e c) -> p e c", e=PAIR)
+
+        def finish_cand(k, z):
+            rows = cand_rows(k * PAIR, PAIR)
+            nc.scalar.copy(out=rows[:, :, 0:D_IN], in_=xt_sb[:, k, :].rearrange("p (e c) -> p e c", e=PAIR))
+            nc.vector.tensor_tensor(
+                out=rows[:, :, D_IN : D_IN + D_STATE],
+                in0=z[:, :, 0:D_STATE],
+                in1=s1_sb[:, k, :].rearrange("p (e c) -> p e c", e=PAIR),
+                op=ALU.mult,
+            )
+            nc.vector.tensor_tensor(
+                out=rows[:, :, D_IN + D_STATE : C],
+                in0=z[:, :, D_STATE : 2 * D_STATE],
+                in1=s2_sb[:, k, :].rearrange("p (e c) -> p e c", e=PAIR),
+                op=ALU.mult,
             )
 
-        def quantise_rows(which, g, codes, scales):
+        def quantise_rows(rows, g, codes, scales):
             grouped = work.tile([P, C * PACK], BF16, name="rows_grouped", tag="rows_grouped", align_bytes=64)
             nc.vector.tensor_copy(
-                out=grouped[:].rearrange("p (c t) -> p c t", t=PACK),
-                in_=term(which, g * PACK, PACK).rearrange("p t c -> p c t"),
+                out=grouped[:].rearrange("p (c t) -> p c t", t=PACK), in_=rows.rearrange("p t c -> p c t")
             )
             nc.vector.quantize_mx(out=codes[:, g, :].bitcast(FP8X4), scales=scales[:, g, :], in_=grouped[:])
 
-        def product_with_a(i, b, rhs_codes, rhs_scales):
-            acc = psum.tile([P, BANK], F32, name="bank", tag="bank")
+        a_codes = []
+        a_scales = []
+
+        def quantise_a_group(a_t):
+            width = PAIR * N_PASSES * P
+            codes = keep.tile([P, width], U32, name="a_codes", tag="a_codes", bufs=12, align_bytes=64)
+            scales = keep.tile([P, width], U8, name="a_scales", tag="a_scales", bufs=12, align_bytes=64)
+            nc.vector.quantize_mx(out=codes[:].bitcast(FP8X4), scales=scales[:], in_=a_t[:])
+            a_codes.append(codes)
+            a_scales.append(scales)
+
+        def product_with_a(m, rhs_codes, rhs_scales):
+            acc = new_bank()
             for e in range(PAIR):
                 for g in range(N_PASSES):
                     cols = slice((e * N_PASSES + g) * P, (e * N_PASSES + g + 1) * P)
                     nc.tensor.matmul_mx(
                         out=acc[:, e * C : (e + 1) * C],
-                        lhsT=a_codes[i][b][:, cols].bitcast(FP8X4),
-                        lhsT_scale=a_scales[i][b][:, cols],
+                        lhsT=a_codes[m][:, cols].bitcast(FP8X4),
+                        lhsT_scale=a_scales[m][:, cols],
                         rhs=rhs_codes[:, g, :].bitcast(FP8X4),
                         rhs_scale=rhs_scales[:, g, :],
                         start=(g == 0),
@@ -110,189 +215,85 @@ def tile_dgggl_pa_kernel(tc, xg_gate, gate_w_z, gate_b_z, xt, state1, state2, su
                     )
             return acc[:].rearrange("p (e c) -> p e c", e=PAIR)
 
-        def first_product(i, b):
-            acc = product_with_a(i, b, cand_codes, cand_scales)
-            nc.scalar.copy(out=term(T1[i], b * PAIR, PAIR), in_=acc)
+        def first_product(m):
+            i, b = divmod(m, N_GROUPS)
+            acc = product_with_a(m, cand_codes, cand_scales)
+            nc.scalar.copy(out=t1_rows(i, b * PAIR, PAIR), in_=acc)
+
+        def quantise_t1(m):
+            i, b = divmod(m, N_GROUPS)
             g, u = divmod(b, GROUPS_PER_PASS)
             if u == GROUPS_PER_PASS - 1:
-                quantise_rows(T1[i], g, t1_codes[i], t1_scales[i])
+                quantise_rows(t1_rows(i, g * PACK, PACK), g, t1_codes[i], t1_scales[i])
 
-        def second_product(i, b):
-            acc = product_with_a(i, b, t1_codes[i], t1_scales[i])
+        t2 = []
+
+        def second_product(m):
+            i, b = divmod(m, N_GROUPS)
+            acc = product_with_a(m, t1_codes[i], t1_scales[i])
+            rows = work.tile([P, PAIR, C], F32, name="t2", tag="t2", bufs=8)
             nc.vector.scalar_tensor_tensor(
-                out=term(T2[i], b * PAIR, PAIR),
+                out=rows[:],
                 in0=acc,
                 scalar=2.0,
-                in1=term(CAND, b * PAIR, PAIR),
+                in1=cand_rows(b * PAIR, PAIR),
                 op0=ALU.mult,
                 op1=ALU.subtract,
             )
+            t2.append(rows)
 
-        with tc.tile_pool(name="stream", bufs=2) as stream:
-            xg_raw = []
-            a_raw = [[], []]
+        n_sources = (1 + SUPPORTS) * N_GROUPS
+        n_a = SUPPORTS * N_GROUPS
+        xg_t = []
+        z_t = []
+        a_t = []
+        second = 0
 
-            def load_xg(k):
-                raw = stream.tile([P, PAIR * F_GATE], BF16, name="xg_raw_%d" % k, tag="xg_raw", bufs=3)
-                nc.sync.dma_start(out=raw[:], in_=xg_groups[k])
-                xg_raw.append(raw)
+        def stores(step):
+            b = step - N_GROUPS - 3
+            if 0 <= b < N_GROUPS:
+                store(CAND, b, cand_t1[:, b * PAIR : (b + 1) * PAIR, :])
+            b = step - 2 * N_GROUPS
+            if 0 <= b < N_GROUPS:
+                store(CAND_AGAIN, b, cand_rows(b * PAIR, PAIR))
+            b = step - 2 * N_GROUPS - 3
+            if 0 <= b < N_GROUPS:
+                store(T1[1], b, t1_rows(1, b * PAIR, PAIR))
 
-            def load_a(i, b):
-                raw = stream.tile([P, PAIR * NODES], BF16, name="a_raw_%d_%d" % (i, b), tag="a_raw", bufs=4)
-                a_groups = supports[i, 0].rearrange("(g r e) m -> g r (e m)", r=P, e=PAIR)
-                nc.sync.dma_start(out=raw[:], in_=a_groups[b])
-                a_raw[i].append(raw)
-
-            load_xg(0)
-            w_sb = keep.tile([P, F_CHUNKS, PAIR * P], BF16)
-            nc.sync.dma_start(out=w_sb[:], in_=gate_w_z.rearrange("(j q e) c -> q j (e c)", q=P, e=PAIR))
-            bias_bf = keep.tile([P, 1], BF16)
-            with nc.allow_non_contiguous_dma(reason="128 bias values, one to a partition"):
-                nc.sync.dma_start(out=bias_bf[:], in_=gate_b_z.rearrange("(c o) -> c o", o=1))
-            load_xg(1)
-            load_a(0, 0)
-            xt_sb = keep.tile([P, N_GROUPS, PAIR * D_IN], BF16)
-            nc.sync.dma_start(out=xt_sb[:], in_=xt[0].rearrange("(g r e) c -> r g (e c)", r=P, e=PAIR))
-            s1_sb = keep.tile([P, N_GROUPS, PAIR * D_STATE], BF16)
-            nc.sync.dma_start(out=s1_sb[:], in_=state1[0].rearrange("(g r e) c -> r g (e c)", r=P, e=PAIR))
-            s2_sb = keep.tile([P, N_GROUPS, PAIR * D_STATE], BF16)
-            nc.sync.dma_start(out=s2_sb[:], in_=state2[0].rearrange("(g r e) c -> r g (e c)", r=P, e=PAIR))
-            for k in range(2, N_GROUPS):
-                load_xg(k)
-                load_a(0, k - 1)
-            load_a(0, N_GROUPS - 1)
-            for b in range(N_GROUPS):
-                load_a(1, b)
-
-            bias = keep.tile([P, 1], F32)
-            nc.vector.tensor_copy(out=bias[:], in_=bias_bf[:])
-
-            def empty_bank(position, run, dst, src):
-                if position == run - 1:
-                    nc.vector.tensor_copy(out=dst, in_=src)
-                else:
-                    nc.scalar.copy(out=dst, in_=src)
-
-            def transpose_xg_group(k):
-                words = xg_raw[k][:].bitcast(F32)
-                xg_t = stream.tile([P, F_CHUNKS * GROUP], F32, name="xg_t", tag="xg_t")
-                n_banks = F_CHUNKS * PAIR // PER_BANK
-                for bank_no in range(n_banks):
-                    bank = psum.tile([P, BANK], F32, name="bank", tag="bank")
-                    for s in range(PER_BANK):
-                        j, e = divmod(bank_no * PER_BANK + s, PAIR)
-                        col = (e * F_CHUNKS + j) * P
-                        nc.tensor.transpose(bank[:, s * P : (s + 1) * P], words[:, col : col + P], ident[:])
-                    empty_bank(bank_no, n_banks, xg_t[:, bank_no * BANK : (bank_no + 1) * BANK], bank[:])
-                return xg_t
-
-            def gate_matmuls(acc, xg_t, quarter):
-                halves = xg_t[:].bitcast(BF16).rearrange("p (j n e) -> p j n e", j=F_CHUNKS, e=PAIR)
-                n_matmuls = F_CHUNKS * PAIR
-                for n in range(quarter * n_matmuls // A_BANKS, (quarter + 1) * n_matmuls // A_BANKS):
-                    j, e = divmod(n, PAIR)
-                    nc.tensor.matmul(
-                        out=acc[:, 0:GROUP],
-                        lhsT=w_sb[:, j, e * P : (e + 1) * P],
-                        rhs=halves[:, j, :, e],
-                        start=(n == 0),
-                        stop=(n == n_matmuls - 1),
-                    )
-
-            def sigmoid(acc):
-                z_t = stream.tile([P, GROUP], F32, name="z_t", tag="z_t")
-                nc.scalar.activation(
-                    out=z_t[:], in_=acc[:, 0:GROUP], func=ACT.Sigmoid, bias=bias[:, 0:1], scale=1.0
-                )
-                return z_t
-
-            def finish_cand(k, z_t):
-                bank = psum.tile([P, BANK], F32, name="bank", tag="bank")
-                for e in range(PAIR):
-                    nc.tensor.transpose(bank[:, e * P : (e + 1) * P], z_t[:, e * P : (e + 1) * P], ident[:])
-                z = bank[:, 0:GROUP].rearrange("p (e c) -> p e c", e=PAIR)
-                rows = term(CAND, k * PAIR, PAIR)
-                nc.scalar.copy(out=rows[:, :, 0:D_IN], in_=xt_sb[:, k, :].rearrange("p (e c) -> p e c", e=PAIR))
-                nc.vector.tensor_tensor(
-                    out=rows[:, :, D_IN : D_IN + D_STATE],
-                    in0=z[:, :, 0:D_STATE],
-                    in1=s1_sb[:, k, :].rearrange("p (e c) -> p e c", e=PAIR),
-                    op=ALU.mult,
-                )
-                nc.vector.tensor_tensor(
-                    out=rows[:, :, D_IN + D_STATE : C],
-                    in0=z[:, :, D_STATE : 2 * D_STATE],
-                    in1=s2_sb[:, k, :].rearrange("p (e c) -> p e c", e=PAIR),
-                    op=ALU.mult,
-                )
+        for step in range(n_sources + 2):
+            if step < N_GROUPS:
+                xg_t.append(transpose_xg_group(step))
+            elif step < n_sources:
+                a_t.append(transpose_a_group(step))
+            k = step - 2
+            if 0 <= k < N_GROUPS:
+                z = turn_z(z_t[k])
+            if 0 <= k + 1 < N_GROUPS:
+                z_t.append(gate(xg_t[k + 1]))
+            if 0 <= k < N_GROUPS:
+                finish_cand(k, z)
                 g, u = divmod(k, GROUPS_PER_PASS)
                 if u == GROUPS_PER_PASS - 1:
-                    quantise_rows(CAND, g, cand_codes, cand_scales)
-
-            a_grouped = {}
-
-            def quantise_a_group(i, b):
-                nc.vector.quantize_mx(
-                    out=a_codes[i][b][:].bitcast(FP8X4), scales=a_scales[i][b][:], in_=a_grouped[(i, b)][:]
-                )
-
-            def transpose_a_bank(i, b, bank_no):
-                if bank_no == 0:
-                    a_grouped[(i, b)] = stream.tile(
-                        [P, PAIR * NODES], BF16, name="a_grouped", tag="a_grouped", bufs=3, align_bytes=64
-                    )
-                words = a_raw[i][b][:].bitcast(F32)
-                grouped_words = a_grouped[(i, b)][:].bitcast(F32).rearrange("p (x r u) -> p x r u", r=P, u=PAIR)
-                bank = psum.tile([P, BANK], F32, name="bank", tag="bank")
-                for s in range(PER_BANK):
-                    col = (bank_no * PER_BANK + s) * P
-                    nc.tensor.transpose(bank[:, s * P : (s + 1) * P], words[:, col : col + P], ident[:])
-                empty_bank(
-                    bank_no,
-                    A_BANKS,
-                    grouped_words[:, bank_no * PAIR : (bank_no + 1) * PAIR, :, :],
-                    bank[:].rearrange("p (x u r) -> p x r u", u=PAIR, r=P),
-                )
-                if bank_no == A_BANKS - 1 and (i, b) != (0, 0):
-                    quantise_a_group(*divmod(i * N_GROUPS + b - 1, N_GROUPS))
-
-            def transpose_a_group(i, b):
-                for bank_no in range(A_BANKS):
-                    transpose_a_bank(i, b, bank_no)
-
-            z_t = {}
-            for k in range(N_GROUPS + 1):
-                if k < N_GROUPS:
-                    xg_t = transpose_xg_group(k)
-                if k > 0:
-                    finish_cand(k - 1, z_t[k - 1])
-                if k < N_GROUPS:
-                    gate_acc = psum.tile([P, BANK], F32, name="bank", tag="bank")
-                for quarter in range(A_BANKS):
-                    if k > 0:
-                        transpose_a_bank(0, k - 1, quarter)
-                    if k < N_GROUPS:
-                        gate_matmuls(gate_acc, xg_t, quarter)
-                if k < N_GROUPS:
-                    z_t[k] = sigmoid(gate_acc)
-            transpose_a_group(1, 0)
-            for b in range(N_GROUPS):
-                if b + 1 < N_GROUPS:
-                    transpose_a_group(1, b + 1)
-                first_product(0, b)
-                store(T1[0], b)
-            quantise_a_group(SUPPORTS - 1, N_GROUPS - 1)
-
-        with tc.tile_pool(name="late", bufs=1) as late:
-            for h in range(1, len(STORES)):
-                out_sb.append(late.tile([P, N_GROUPS * PAIR, len(STORES[h]) * C], F32, name="out_sb_%d" % h))
-            for b in range(N_GROUPS):
-                first_product(1, b)
-                store(T1[1], b)
-                nc.scalar.copy(out=term(CAND_AGAIN, b * PAIR, PAIR), in_=term(CAND, b * PAIR, PAIR))
-            for b in range(N_GROUPS):
-                second_product(0, b)
-                store(T2[0], b)
-            for b in range(N_GROUPS):
-                second_product(1, b)
-                store(T2[1], b)
+                    quantise_rows(cand_rows(g * PACK, PACK), g, cand_codes, cand_scales)
+            m = step - N_GROUPS - 1
+            if 0 <= m < n_a:
+                quantise_a_group(a_t[m])
+            if 0 <= m - 2 < n_a:
+                quantise_t1(m - 2)
+            stores(step)
+            if step + RAW_BUFS < n_sources:
+                load(step + RAW_BUFS)
+            if 0 <= m - 1 < n_a:
+                first_product(m - 1)
+            if step == n_sources + 1:
+                quantise_t1(n_a - 1)
+                store(T1[1], N_GROUPS - 1, t1_rows(1, (N_GROUPS - 1) * PAIR, PAIR))
+            if m - 1 >= N_GROUPS + 1 and second < N_GROUPS:
+                second_product(second)
+                store(T2[0], second, t2[second][:])
+                second += 1
+        while second < n_a:
+            second_product(second)
+            i, b = divmod(second, N_GROUPS)
+            store(T2[i], b, t2[second][:])
+            second += 1

@@ -1,4 +1,5 @@
 from contextlib import ExitStack
+from functools import partial
 
 import concourse.mybir as mybir
 from concourse.masks import make_identity
@@ -28,12 +29,19 @@ C = D_IN + 2 * D_STATE
 BANK = 512
 PER_BANK = BANK // P
 A_BANKS = NODES // BANK
+GATE_MATMULS = F_CHUNKS * PAIR
+XG_BANKS = F_CHUNKS * PAIR // PER_BANK
 CAND = 0
 CAND_AGAIN = 3
 T1 = (1, 4)
 T2 = (2, 5)
 
+FIRST_PARTS = 2
+OPENED = 2
 RAW_BUFS = 6
+FIRST_A_STEP = 4
+A_BANKS_PER_STEP = 3
+BANKS_PER_PRODUCT = 3
 
 FLOPS = 2 * NODES * F_GATE * P + 2 * SUPPORTS * 2 * NODES * NODES * C
 
@@ -48,7 +56,7 @@ def tile_dgggl_pa_kernel(tc, xg_gate, gate_w_z, gate_b_z, xt, state1, state2, su
     with ExitStack() as ctx:
         keep = ctx.enter_context(tc.tile_pool(name="keep", bufs=1))
         work = ctx.enter_context(tc.tile_pool(name="work", bufs=2))
-        psum = ctx.enter_context(tc.psum_pool(name="psum", bufs=8))
+        psum = ctx.enter_context(tc.psum_pool(name="psum", bufs=1))
         ctx.enter_context(tc.manual_schedule())
 
         ident = keep.tile([P, P], F32)
@@ -78,61 +86,84 @@ def tile_dgggl_pa_kernel(tc, xg_gate, gate_w_z, gate_b_z, xt, state1, state2, su
             col = first_term * C
             nc.sync.dma_start(out=out_groups[b][:, :, col : col + rows.shape[2]], in_=rows)
 
-        raw = []
+        with tc.tile_pool(name="gate_pool", bufs=1) as gate_pool:
+            sources = []
+            m = 0
+            for k in range(N_GROUPS):
+                sources.append((0, k))
+                while m * A_BANKS < (k + 1 - FIRST_A_STEP) * A_BANKS_PER_STEP:
+                    sources.append((1, m))
+                    m += 1
+            sources.extend([(1, later) for later in range(m, SUPPORTS * N_GROUPS)])
+            raw = {}
 
-        def load(n):
-            kind, b = divmod(n, N_GROUPS)
-            width = PAIR * (F_GATE if kind == 0 else NODES)
-            tile_n = work.tile([P, width], BF16, name="raw_%d" % n, tag="raw", bufs=RAW_BUFS, align_bytes=64)
-            nc.sync.dma_start(out=tile_n[:], in_=xg_groups[b] if kind == 0 else a_groups[kind - 1][b])
-            raw.append(tile_n)
+            def load_next():
+                n = len(raw)
+                if n == len(sources):
+                    return
+                kind, k = sources[n]
+                width = PAIR * (F_GATE if kind == 0 else NODES)
+                tile_n = work.tile([P, width], BF16, name="raw_%d" % n, tag="raw", bufs=RAW_BUFS, align_bytes=64)
+                i, b = divmod(k, N_GROUPS)
+                for part in range(FIRST_PARTS if n == 0 else 1):
+                    cols = slice(part * width // FIRST_PARTS, (part + 1) * width // FIRST_PARTS) if n == 0 else slice(0, width)
+                    nc.sync.dma_start(out=tile_n[:, cols], in_=(xg_groups[k] if kind == 0 else a_groups[i][b])[:, cols])
+                raw[(kind, k)] = tile_n
 
-        load(0)
-        w_sb = keep.tile([P, F_CHUNKS, PAIR * P], BF16)
-        nc.sync.dma_start(out=w_sb[:], in_=gate_w_z.rearrange("(j q e) c -> q j (e c)", q=P, e=PAIR))
-        bias_bf = keep.tile([P, 1], BF16)
-        with nc.allow_non_contiguous_dma(reason="128 bias values, one to a partition"):
-            nc.sync.dma_start(out=bias_bf[:], in_=gate_b_z.rearrange("(c o) -> c o", o=1))
-        load(1)
-        xt_sb = keep.tile([P, N_GROUPS, PAIR * D_IN], BF16)
-        nc.sync.dma_start(out=xt_sb[:], in_=xt[0].rearrange("(g r e) c -> r g (e c)", r=P, e=PAIR))
-        s1_sb = keep.tile([P, N_GROUPS, PAIR * D_STATE], BF16)
-        nc.sync.dma_start(out=s1_sb[:], in_=state1[0].rearrange("(g r e) c -> r g (e c)", r=P, e=PAIR))
-        s2_sb = keep.tile([P, N_GROUPS, PAIR * D_STATE], BF16)
-        nc.sync.dma_start(out=s2_sb[:], in_=state2[0].rearrange("(g r e) c -> r g (e c)", r=P, e=PAIR))
-        for n in range(2, RAW_BUFS):
-            load(n)
+            load_next()
+            w_sb = gate_pool.tile([P, F_CHUNKS, PAIR * P], BF16)
+            nc.sync.dma_start(out=w_sb[:], in_=gate_w_z.rearrange("(j q e) c -> q j (e c)", q=P, e=PAIR))
+            bias_bf = gate_pool.tile([P, 1], BF16)
+            with nc.allow_non_contiguous_dma(reason="128 bias values, one to a partition"):
+                nc.sync.dma_start(out=bias_bf[:], in_=gate_b_z.rearrange("(c o) -> c o", o=1))
+            load_next()
+            load_next()
+            xt_sb = gate_pool.tile([P, N_GROUPS, PAIR * D_IN], BF16)
+            nc.sync.dma_start(out=xt_sb[:], in_=xt[0].rearrange("(g r e) c -> r g (e c)", r=P, e=PAIR))
+            s1_sb = gate_pool.tile([P, N_GROUPS, PAIR * D_STATE], BF16)
+            nc.sync.dma_start(out=s1_sb[:], in_=state1[0].rearrange("(g r e) c -> r g (e c)", r=P, e=PAIR))
+            s2_sb = gate_pool.tile([P, N_GROUPS, PAIR * D_STATE], BF16)
+            nc.sync.dma_start(out=s2_sb[:], in_=state2[0].rearrange("(g r e) c -> r g (e c)", r=P, e=PAIR))
+            while len(raw) < RAW_BUFS:
+                load_next()
 
-        bias = keep.tile([P, 1], F32)
-        nc.vector.tensor_copy(out=bias[:], in_=bias_bf[:])
+            bias = gate_pool.tile([P, 1], F32)
+            nc.vector.tensor_copy(out=bias[:], in_=bias_bf[:])
 
-        def new_bank():
-            return psum.tile([P, BANK], F32, name="bank", tag="bank")
+            def turn_bank():
+                return psum.tile([P, BANK], F32, name="turn_bank", tag="turn_bank", bufs=4)
 
-        def empty_bank(position, dst, src):
-            if position == 0:
-                nc.vector.tensor_copy(out=dst, in_=src)
-            else:
-                nc.scalar.copy(out=dst, in_=src)
+            def sum_bank():
+                return psum.tile([P, BANK], F32, name="sum_bank", tag="sum_bank", bufs=4)
 
-        def transpose_xg_group(k):
-            words = raw[k][:].bitcast(F32)
-            xg_t = work.tile([P, F_CHUNKS * GROUP], F32, name="xg_t", tag="turned", bufs=3, align_bytes=64)
-            for bank_no in range(F_CHUNKS * PAIR // PER_BANK):
-                bank = new_bank()
+            def empty_bank(position, dst, src):
+                if position == 0:
+                    nc.vector.tensor_copy(out=dst, in_=src)
+                else:
+                    nc.scalar.copy(out=dst, in_=src)
+
+            xg_t = {}
+
+            def transpose_xg_bank(k, bank_no):
+                if bank_no == 0:
+                    xg_t[k] = gate_pool.tile([P, F_CHUNKS * GROUP * PAIR], BF16, name="xg_t", tag="xg_t", bufs=2)
+                words = raw[(0, k)][:].bitcast(F32)
+                bank = turn_bank()
                 for s in range(PER_BANK):
-                    j, e = divmod(bank_no * PER_BANK + s, PAIR)
-                    col = (e * F_CHUNKS + j) * P
+                    col = (bank_no * PER_BANK + s) * P
                     nc.tensor.transpose(bank[:, s * P : (s + 1) * P], words[:, col : col + P], ident[:])
-                empty_bank(bank_no, xg_t[:, bank_no * BANK : (bank_no + 1) * BANK], bank[:])
-            return xg_t
+                empty_bank(bank_no, xg_t[k][:].bitcast(F32)[:, bank_no * BANK : (bank_no + 1) * BANK], bank[:])
+                if bank_no == XG_BANKS - 1:
+                    load_next()
 
-        def transpose_a_group(n):
-            words = raw[n][:].bitcast(F32)
-            a_t = work.tile([P, PAIR * NODES], BF16, name="a_t", tag="turned", bufs=3, align_bytes=64)
-            a_t_words = a_t[:].bitcast(F32).rearrange("p (x r u) -> p x r u", r=P, u=PAIR)
-            for bank_no in range(A_BANKS):
-                bank = new_bank()
+            a_t = {}
+
+            def transpose_a_bank(m, bank_no):
+                if bank_no == 0:
+                    a_t[m] = work.tile([P, PAIR * NODES], BF16, name="a_t", tag="a_t", bufs=3, align_bytes=64)
+                words = raw[(1, m)][:].bitcast(F32)
+                a_t_words = a_t[m][:].bitcast(F32).rearrange("p (x r u) -> p x r u", r=P, u=PAIR)
+                bank = turn_bank()
                 for s in range(PER_BANK):
                     col = (bank_no * PER_BANK + s) * P
                     nc.tensor.transpose(bank[:, s * P : (s + 1) * P], words[:, col : col + P], ident[:])
@@ -141,71 +172,71 @@ def tile_dgggl_pa_kernel(tc, xg_gate, gate_w_z, gate_b_z, xt, state1, state2, su
                     a_t_words[:, bank_no * PAIR : (bank_no + 1) * PAIR, :, :],
                     bank[:].rearrange("p (x u r) -> p x r u", u=PAIR, r=P),
                 )
-            return a_t
+                if bank_no == A_BANKS - 1:
+                    load_next()
 
-        def gate(xg_t):
-            acc = new_bank()
-            halves = xg_t[:].bitcast(BF16).rearrange("p (j n e) -> p j n e", j=F_CHUNKS, e=PAIR)
-            for j in range(F_CHUNKS):
-                for e in range(PAIR):
+            def gate_matmuls(acc, k, first, last):
+                halves = xg_t[k][:].rearrange("p (e j r h) -> p j h e r", e=PAIR, j=F_CHUNKS, h=PAIR)
+                for n in range(first, last):
+                    j, h = divmod(n, PAIR)
                     nc.tensor.matmul(
-                        out=acc[:, 0:GROUP],
-                        lhsT=w_sb[:, j, e * P : (e + 1) * P],
-                        rhs=halves[:, j, :, e],
-                        start=(j == 0 and e == 0),
-                        stop=(j == F_CHUNKS - 1 and e == PAIR - 1),
+                        out=acc[:, 0:GROUP].rearrange("p (e r) -> p e r", e=PAIR),
+                        lhsT=w_sb[:, j, h * P : (h + 1) * P],
+                        rhs=halves[:, j, h, :, :],
+                        start=(n == 0),
+                        stop=(n == GATE_MATMULS - 1),
                     )
-            z_t = work.tile([P, GROUP], F32, name="z_t", tag="z_t")
-            nc.scalar.activation(out=z_t[:], in_=acc[:, 0:GROUP], func=ACT.Sigmoid, bias=bias[:, 0:1], scale=1.0)
-            return z_t
 
-        def turn_z(z_t):
-            bank = new_bank()
-            for e in range(PAIR):
-                nc.tensor.transpose(bank[:, e * P : (e + 1) * P], z_t[:, e * P : (e + 1) * P], ident[:])
-            return bank[:, 0:GROUP].rearrange("p (e c) -> p e c", e=PAIR)
+            def sigmoid(acc):
+                z_t = gate_pool.tile([P, GROUP], F32, name="z_t", tag="z_t", bufs=2)
+                nc.scalar.activation(out=z_t[:], in_=acc[:, 0:GROUP], func=ACT.Sigmoid, bias=bias[:, 0:1], scale=1.0)
+                return z_t
 
-        def finish_cand(k, z):
-            rows = cand_rows(k * PAIR, PAIR)
-            nc.scalar.copy(out=rows[:, :, 0:D_IN], in_=xt_sb[:, k, :].rearrange("p (e c) -> p e c", e=PAIR))
-            nc.vector.tensor_tensor(
-                out=rows[:, :, D_IN : D_IN + D_STATE],
-                in0=z[:, :, 0:D_STATE],
-                in1=s1_sb[:, k, :].rearrange("p (e c) -> p e c", e=PAIR),
-                op=ALU.mult,
-            )
-            nc.vector.tensor_tensor(
-                out=rows[:, :, D_IN + D_STATE : C],
-                in0=z[:, :, D_STATE : 2 * D_STATE],
-                in1=s2_sb[:, k, :].rearrange("p (e c) -> p e c", e=PAIR),
-                op=ALU.mult,
-            )
+            def turn_z(z_t):
+                bank = sum_bank()
+                for e in range(PAIR):
+                    nc.tensor.transpose(bank[:, e * P : (e + 1) * P], z_t[:, e * P : (e + 1) * P], ident[:])
+                return bank[:, 0:GROUP].rearrange("p (e c) -> p e c", e=PAIR)
 
-        def quantise_rows(rows, g, codes, scales):
-            grouped = work.tile([P, C * PACK], BF16, name="rows_grouped", tag="rows_grouped", align_bytes=64)
-            nc.vector.tensor_copy(
-                out=grouped[:].rearrange("p (c t) -> p c t", t=PACK), in_=rows.rearrange("p t c -> p c t")
-            )
-            nc.vector.quantize_mx(out=codes[:, g, :].bitcast(FP8X4), scales=scales[:, g, :], in_=grouped[:])
+            def finish_cand(k, z):
+                rows = cand_rows(k * PAIR, PAIR)
+                nc.scalar.copy(out=rows[:, :, 0:D_IN], in_=xt_sb[:, k, :].rearrange("p (e c) -> p e c", e=PAIR))
+                nc.vector.tensor_tensor(
+                    out=rows[:, :, D_IN : D_IN + D_STATE],
+                    in0=z[:, :, 0:D_STATE],
+                    in1=s1_sb[:, k, :].rearrange("p (e c) -> p e c", e=PAIR),
+                    op=ALU.mult,
+                )
+                nc.vector.tensor_tensor(
+                    out=rows[:, :, D_IN + D_STATE : C],
+                    in0=z[:, :, D_STATE : 2 * D_STATE],
+                    in1=s2_sb[:, k, :].rearrange("p (e c) -> p e c", e=PAIR),
+                    op=ALU.mult,
+                )
 
-        a_codes = []
-        a_scales = []
+            def quantise_rows(rows, g, codes, scales):
+                grouped = work.tile([P, C * PACK], BF16, name="rows_grouped", tag="rows_grouped", align_bytes=64)
+                nc.vector.tensor_copy(
+                    out=grouped[:].rearrange("p (c t) -> p c t", t=PACK), in_=rows.rearrange("p t c -> p c t")
+                )
+                nc.vector.quantize_mx(out=codes[:, g, :].bitcast(FP8X4), scales=scales[:, g, :], in_=grouped[:])
 
-        def quantise_a_group(a_t):
-            width = PAIR * N_PASSES * P
-            codes = keep.tile([P, width], U32, name="a_codes", tag="a_codes", bufs=12, align_bytes=64)
-            scales = keep.tile([P, width], U8, name="a_scales", tag="a_scales", bufs=12, align_bytes=64)
-            nc.vector.quantize_mx(out=codes[:].bitcast(FP8X4), scales=scales[:], in_=a_t[:])
-            a_codes.append(codes)
-            a_scales.append(scales)
+            a_codes = []
+            a_scales = []
 
-        def product_with_a(m, rhs_codes, rhs_scales):
-            acc = new_bank()
-            for e in range(PAIR):
-                for g in range(N_PASSES):
+            def quantise_a_group(m):
+                width = PAIR * N_PASSES * P
+                codes = keep.tile([P, width], U32, name="a_codes", tag="a_codes", bufs=12, align_bytes=64)
+                scales = keep.tile([P, width], U8, name="a_scales", tag="a_scales", bufs=12, align_bytes=64)
+                nc.vector.quantize_mx(out=codes[:].bitcast(FP8X4), scales=scales[:], in_=a_t[m][:])
+                a_codes.append(codes)
+                a_scales.append(scales)
+
+            def multiply(acc, m, e, passes, rhs_codes, rhs_scales):
+                for g in passes:
                     cols = slice((e * N_PASSES + g) * P, (e * N_PASSES + g + 1) * P)
                     nc.tensor.matmul_mx(
-                        out=acc[:, e * C : (e + 1) * C],
+                        out=acc,
                         lhsT=a_codes[m][:, cols].bitcast(FP8X4),
                         lhsT_scale=a_scales[m][:, cols],
                         rhs=rhs_codes[:, g, :].bitcast(FP8X4),
@@ -213,87 +244,140 @@ def tile_dgggl_pa_kernel(tc, xg_gate, gate_w_z, gate_b_z, xt, state1, state2, su
                         start=(g == 0),
                         stop=(g == N_PASSES - 1),
                     )
-            return acc[:].rearrange("p (e c) -> p e c", e=PAIR)
 
-        def first_product(m):
-            i, b = divmod(m, N_GROUPS)
-            acc = product_with_a(m, cand_codes, cand_scales)
-            nc.scalar.copy(out=t1_rows(i, b * PAIR, PAIR), in_=acc)
+            def product_with_a(m, rhs_codes, rhs_scales):
+                acc = sum_bank()
+                for e in range(PAIR):
+                    multiply(acc[:, e * C : (e + 1) * C], m, e, range(N_PASSES), rhs_codes, rhs_scales)
+                return acc[:].rearrange("p (e c) -> p e c", e=PAIR)
 
-        def quantise_t1(m):
-            i, b = divmod(m, N_GROUPS)
-            g, u = divmod(b, GROUPS_PER_PASS)
-            if u == GROUPS_PER_PASS - 1:
-                quantise_rows(t1_rows(i, g * PACK, PACK), g, t1_codes[i], t1_scales[i])
+            def first_product(m):
+                i, b = divmod(m, N_GROUPS)
+                acc = product_with_a(m, cand_codes, cand_scales)
+                nc.scalar.copy(out=t1_rows(i, b * PAIR, PAIR), in_=acc)
 
-        t2 = []
+            def open_first_product(m):
+                accs = []
+                for e in range(PAIR):
+                    accs.append(sum_bank()[:, 0:C])
+                    multiply(accs[e], m, e, range(N_PASSES - 1), cand_codes, cand_scales)
+                return accs
 
-        def second_product(m):
-            i, b = divmod(m, N_GROUPS)
-            acc = product_with_a(m, t1_codes[i], t1_scales[i])
-            rows = work.tile([P, PAIR, C], F32, name="t2", tag="t2", bufs=8)
-            nc.vector.scalar_tensor_tensor(
-                out=rows[:],
-                in0=acc,
-                scalar=2.0,
-                in1=cand_rows(b * PAIR, PAIR),
-                op0=ALU.mult,
-                op1=ALU.subtract,
-            )
-            t2.append(rows)
+            def close_first_product(m, accs):
+                i, b = divmod(m, N_GROUPS)
+                for e in range(PAIR):
+                    multiply(accs[e], m, e, range(N_PASSES - 1, N_PASSES), cand_codes, cand_scales)
+                    nc.scalar.copy(out=t1_rows(i, b * PAIR + e, 1)[:, 0, :], in_=accs[e])
 
-        n_sources = (1 + SUPPORTS) * N_GROUPS
-        n_a = SUPPORTS * N_GROUPS
-        xg_t = []
-        z_t = []
-        a_t = []
-        second = 0
-
-        def stores(step):
-            b = step - N_GROUPS - 3
-            if 0 <= b < N_GROUPS:
-                store(CAND, b, cand_t1[:, b * PAIR : (b + 1) * PAIR, :])
-            b = step - 2 * N_GROUPS
-            if 0 <= b < N_GROUPS:
-                store(CAND_AGAIN, b, cand_rows(b * PAIR, PAIR))
-            b = step - 2 * N_GROUPS - 3
-            if 0 <= b < N_GROUPS:
-                store(T1[1], b, t1_rows(1, b * PAIR, PAIR))
-
-        for step in range(n_sources + 2):
-            if step < N_GROUPS:
-                xg_t.append(transpose_xg_group(step))
-            elif step < n_sources:
-                a_t.append(transpose_a_group(step))
-            k = step - 2
-            if 0 <= k < N_GROUPS:
-                z = turn_z(z_t[k])
-            if 0 <= k + 1 < N_GROUPS:
-                z_t.append(gate(xg_t[k + 1]))
-            if 0 <= k < N_GROUPS:
-                finish_cand(k, z)
-                g, u = divmod(k, GROUPS_PER_PASS)
+            def quantise_t1(m):
+                i, b = divmod(m, N_GROUPS)
+                g, u = divmod(b, GROUPS_PER_PASS)
                 if u == GROUPS_PER_PASS - 1:
-                    quantise_rows(cand_rows(g * PACK, PACK), g, cand_codes, cand_scales)
-            m = step - N_GROUPS - 1
-            if 0 <= m < n_a:
-                quantise_a_group(a_t[m])
-            if 0 <= m - 2 < n_a:
-                quantise_t1(m - 2)
-            stores(step)
-            if step + RAW_BUFS < n_sources:
-                load(step + RAW_BUFS)
-            if 0 <= m - 1 < n_a:
-                first_product(m - 1)
-            if step == n_sources + 1:
-                quantise_t1(n_a - 1)
-                store(T1[1], N_GROUPS - 1, t1_rows(1, (N_GROUPS - 1) * PAIR, PAIR))
-            if m - 1 >= N_GROUPS + 1 and second < N_GROUPS:
-                second_product(second)
-                store(T2[0], second, t2[second][:])
-                second += 1
-        while second < n_a:
-            second_product(second)
-            i, b = divmod(second, N_GROUPS)
-            store(T2[i], b, t2[second][:])
-            second += 1
+                    quantise_rows(t1_rows(i, g * PACK, PACK), g, t1_codes[i], t1_scales[i])
+
+            t2 = []
+
+            def second_product(m):
+                i, b = divmod(m, N_GROUPS)
+                acc = product_with_a(m, t1_codes[i], t1_scales[i])
+                rows = late.tile([P, PAIR, C], F32, name="t2", tag="t2", bufs=8)
+                nc.vector.scalar_tensor_tensor(
+                    out=rows[:],
+                    in0=acc,
+                    scalar=2.0,
+                    in1=cand_rows(b * PAIR, PAIR),
+                    op0=ALU.mult,
+                    op1=ALU.subtract,
+                )
+                t2.append(rows)
+
+            pending = []
+
+            def flush():
+                while pending:
+                    pending.pop(0)()
+
+            a_banks = [(m, bank_no) for m in range(SUPPORTS * N_GROUPS) for bank_no in range(A_BANKS)]
+
+            def turn_a():
+                if a_banks:
+                    m, bank_no = a_banks.pop(0)
+                    transpose_a_bank(m, bank_no)
+                    if bank_no == A_BANKS - 1:
+                        pending.append(partial(quantise_a_group, m))
+
+            z_t = {}
+            for k in range(N_GROUPS + 1):
+                banks = []
+                if k < N_GROUPS:
+                    banks.extend([partial(transpose_xg_bank, k, bank_no) for bank_no in range(XG_BANKS)])
+                if k >= FIRST_A_STEP:
+                    for n in range(A_BANKS_PER_STEP if k < N_GROUPS else XG_BANKS + A_BANKS_PER_STEP):
+                        banks.insert(min(2 * n + 1, len(banks)), turn_a)
+                gating = k - 2
+                multiplying = 0 <= k - 1
+                if multiplying:
+                    acc = sum_bank()
+                for n, bank in enumerate(banks):
+                    if k == 1:
+                        gate_matmuls(acc, k - 1, n * GATE_MATMULS // len(banks), (n + 1) * GATE_MATMULS // len(banks))
+                    bank()
+                    if n == 1:
+                        flush()
+                        if gating >= 0:
+                            z = turn_z(z_t[gating])
+                    if k > 1:
+                        gate_matmuls(acc, k - 1, n * GATE_MATMULS // len(banks), (n + 1) * GATE_MATMULS // len(banks))
+                    if n == 2 and gating >= 0:
+                        finish_cand(gating, z)
+                if multiplying:
+                    z_t[k - 1] = sigmoid(acc)
+                g, u = divmod(gating, GROUPS_PER_PASS)
+                if gating >= 0 and u == GROUPS_PER_PASS - 1:
+                    pending.append(partial(quantise_rows, cand_rows(g * PACK, PACK), g, cand_codes, cand_scales))
+            def give_a_run():
+                for n in range(BANKS_PER_PRODUCT):
+                    turn_a()
+                    if n == 0:
+                        flush()
+
+            give_a_run()
+            finish_cand(N_GROUPS - 1, turn_z(z_t[N_GROUPS - 1]))
+            quantise_rows(cand_rows(NODES // P - PACK, PACK), N_PASSES - 1, cand_codes, cand_scales)
+            opened = []
+            for m in range(OPENED):
+                opened.append(open_first_product(m))
+                if m < OPENED - 1:
+                    give_a_run()
+
+        late = ctx.enter_context(tc.tile_pool(name="late", bufs=1))
+        firsts = [[(first_product, i * N_GROUPS + b) for b in range(N_GROUPS)] for i in range(SUPPORTS)]
+        seconds = [[(second_product, i * N_GROUPS + b) for b in range(N_GROUPS)] for i in range(SUPPORTS)]
+        held = 3
+        products = firsts[0] + firsts[1][:1] + seconds[0][:-held] + firsts[1][1:] + seconds[0][-held:] + seconds[1]
+        stores = []
+        again = 0
+        for n, (product, p) in enumerate(products):
+            if n >= OPENED:
+                give_a_run()
+                flush()
+            for give in stores:
+                give()
+            stores = []
+            if N_GROUPS < n <= 2 * N_GROUPS:
+                store(CAND_AGAIN, again, cand_rows(again * PAIR, PAIR))
+                again += 1
+            if n < OPENED:
+                close_first_product(p, opened[p])
+            else:
+                product(p)
+            i, b = divmod(p, N_GROUPS)
+            if product is first_product:
+                if b % GROUPS_PER_PASS == GROUPS_PER_PASS - 1:
+                    pending.append(partial(quantise_t1, p))
+                rows = cand_t1[:, b * PAIR : (b + 1) * PAIR, :] if i == 0 else t1_rows(i, b * PAIR, PAIR)
+                stores.append(partial(store, CAND if i == 0 else T1[i], b, rows))
+            else:
+                stores.append(partial(store, T2[i], b, t2[p][:]))
+        for give in stores:
+            give()

@@ -32,7 +32,6 @@ A_BANKS = NODES // BANK
 GATE_MATMULS = F_CHUNKS * PAIR
 XG_BANKS = F_CHUNKS * PAIR // PER_BANK
 CAND = 0
-CAND_AGAIN = 3
 T1 = (1, 4)
 T2 = (2, 5)
 
@@ -280,9 +279,12 @@ def tile_dgggl_pa_kernel(tc, xg_gate, gate_w_z, gate_b_z, xt, state1, state2, su
             def second_product(m):
                 i, b = divmod(m, N_GROUPS)
                 acc = product_with_a(m, t1_codes[i], t1_scales[i])
-                rows = late.tile([P, PAIR, C], F32, name="t2", tag="t2", bufs=8)
+                width = C * PAIR if i == 0 else C
+                rows = late.tile([P, PAIR, width], F32, name="t2_%d" % i, tag="t2_%d" % i, bufs=4)
+                if i == 0:
+                    nc.scalar.copy(out=rows[:, :, C : 2 * C], in_=cand_rows(b * PAIR, PAIR))
                 nc.vector.scalar_tensor_tensor(
-                    out=rows[:],
+                    out=rows[:, :, 0:C],
                     in0=acc,
                     scalar=2.0,
                     in1=cand_rows(b * PAIR, PAIR),
@@ -356,7 +358,6 @@ def tile_dgggl_pa_kernel(tc, xg_gate, gate_w_z, gate_b_z, xt, state1, state2, su
         held = 3
         products = firsts[0] + firsts[1][:1] + seconds[0][:-held] + firsts[1][1:] + seconds[0][-held:] + seconds[1]
         stores = []
-        again = 0
         for n, (product, p) in enumerate(products):
             if n >= OPENED:
                 give_a_run()
@@ -364,9 +365,6 @@ def tile_dgggl_pa_kernel(tc, xg_gate, gate_w_z, gate_b_z, xt, state1, state2, su
             for give in stores:
                 give()
             stores = []
-            if N_GROUPS < n <= 2 * N_GROUPS:
-                store(CAND_AGAIN, again, cand_rows(again * PAIR, PAIR))
-                again += 1
             if n < OPENED:
                 close_first_product(p, opened[p])
             else:

@@ -38,9 +38,14 @@ T2 = (2, 5)
 FIRST_PARTS = 2
 OPENED = 2
 RAW_BUFS = 6
-FIRST_A_STEP = 4
+SMALL_AFTER = 5
+FIRST_GATING_STEP = 4
+LAST_STEP_BANKS = 6
+FIRST_A_STEP = 7
 A_BANKS_PER_STEP = 3
-BANKS_PER_PRODUCT = 3
+RUN_BANKS = 4
+RUN_PRODUCTS = 1
+GATE_RUN = 3
 
 FLOPS = 2 * NODES * F_GATE * P + 2 * SUPPORTS * 2 * NODES * NODES * C
 
@@ -90,7 +95,7 @@ def tile_dgggl_pa_kernel(tc, xg_gate, gate_w_z, gate_b_z, xt, state1, state2, su
             m = 0
             for k in range(N_GROUPS):
                 sources.append((0, k))
-                while m * A_BANKS < (k + 1 - FIRST_A_STEP) * A_BANKS_PER_STEP:
+                while m < SUPPORTS * N_GROUPS and m * A_BANKS < (k + 1 - FIRST_A_STEP) * A_BANKS_PER_STEP:
                     sources.append((1, m))
                     m += 1
             sources.extend([(1, later) for later in range(m, SUPPORTS * N_GROUPS)])
@@ -117,6 +122,8 @@ def tile_dgggl_pa_kernel(tc, xg_gate, gate_w_z, gate_b_z, xt, state1, state2, su
                 nc.sync.dma_start(out=bias_bf[:], in_=gate_b_z.rearrange("(c o) -> c o", o=1))
             load_next()
             load_next()
+            while len(raw) < SMALL_AFTER:
+                load_next()
             xt_sb = gate_pool.tile([P, N_GROUPS, PAIR * D_IN], BF16)
             nc.sync.dma_start(out=xt_sb[:], in_=xt[0].rearrange("(g r e) c -> r g (e c)", r=P, e=PAIR))
             s1_sb = gate_pool.tile([P, N_GROUPS, PAIR * D_STATE], BF16)
@@ -187,7 +194,7 @@ def tile_dgggl_pa_kernel(tc, xg_gate, gate_w_z, gate_b_z, xt, state1, state2, su
                     )
 
             def sigmoid(acc):
-                z_t = gate_pool.tile([P, GROUP], F32, name="z_t", tag="z_t", bufs=2)
+                z_t = gate_pool.tile([P, GROUP], F32, name="z_t", tag="z_t", bufs=4)
                 nc.scalar.activation(out=z_t[:], in_=acc[:, 0:GROUP], func=ACT.Sigmoid, bias=bias[:, 0:1], scale=1.0)
                 return z_t
 
@@ -293,6 +300,22 @@ def tile_dgggl_pa_kernel(tc, xg_gate, gate_w_z, gate_b_z, xt, state1, state2, su
                 )
                 t2.append(rows)
 
+            def last_product(m):
+                i, b = divmod(m, N_GROUPS)
+                rows = late.tile([P, PAIR, C], F32, name="t2_%d" % i, tag="t2_%d" % i, bufs=4)
+                for e in range(PAIR):
+                    acc = sum_bank()[:, 0:C]
+                    multiply(acc, m, e, range(N_PASSES), t1_codes[i], t1_scales[i])
+                    nc.vector.scalar_tensor_tensor(
+                        out=rows[:, e, :],
+                        in0=acc,
+                        scalar=2.0,
+                        in1=cand_rows(b * PAIR + e, 1)[:, 0, :],
+                        op0=ALU.mult,
+                        op1=ALU.subtract,
+                    )
+                    nc.sync.dma_start(out=out_groups[b][:, e, T2[i] * C : (T2[i] + 1) * C], in_=rows[:, e, :])
+
             pending = []
 
             def flush():
@@ -309,14 +332,18 @@ def tile_dgggl_pa_kernel(tc, xg_gate, gate_w_z, gate_b_z, xt, state1, state2, su
                         pending.append(partial(quantise_a_group, m))
 
             z_t = {}
+            gated = 0
             for k in range(N_GROUPS + 1):
                 banks = []
                 if k < N_GROUPS:
                     banks.extend([partial(transpose_xg_bank, k, bank_no) for bank_no in range(XG_BANKS)])
                 if k >= FIRST_A_STEP:
-                    for n in range(A_BANKS_PER_STEP if k < N_GROUPS else XG_BANKS + A_BANKS_PER_STEP):
+                    for n in range(A_BANKS_PER_STEP if k < N_GROUPS else LAST_STEP_BANKS):
                         banks.insert(min(2 * n + 1, len(banks)), turn_a)
-                gating = k - 2
+                gating = []
+                while k >= FIRST_GATING_STEP and len(gating) < 2 and gated < k - 1:
+                    gating.append(gated)
+                    gated += 1
                 multiplying = 0 <= k - 1
                 if multiplying:
                     acc = sum_bank()
@@ -326,24 +353,25 @@ def tile_dgggl_pa_kernel(tc, xg_gate, gate_w_z, gate_b_z, xt, state1, state2, su
                     bank()
                     if n == 1:
                         flush()
-                        if gating >= 0:
-                            z = turn_z(z_t[gating])
+                        z = [turn_z(z_t[group]) for group in gating]
                     if k > 1:
                         gate_matmuls(acc, k - 1, n * GATE_MATMULS // len(banks), (n + 1) * GATE_MATMULS // len(banks))
-                    if n == 2 and gating >= 0:
-                        finish_cand(gating, z)
+                    if n == 2:
+                        for group, z_group in zip(gating, z):
+                            finish_cand(group, z_group)
                 if multiplying:
                     z_t[k - 1] = sigmoid(acc)
-                g, u = divmod(gating, GROUPS_PER_PASS)
-                if gating >= 0 and u == GROUPS_PER_PASS - 1:
-                    pending.append(partial(quantise_rows, cand_rows(g * PACK, PACK), g, cand_codes, cand_scales))
-            def give_a_run():
-                for n in range(BANKS_PER_PRODUCT):
+                for group in gating:
+                    g, u = divmod(group, GROUPS_PER_PASS)
+                    if u == GROUPS_PER_PASS - 1:
+                        pending.append(partial(quantise_rows, cand_rows(g * PACK, PACK), g, cand_codes, cand_scales))
+            def give_a_run(banks=RUN_BANKS):
+                for n in range(banks):
                     turn_a()
                     if n == 0:
                         flush()
 
-            give_a_run()
+            give_a_run(GATE_RUN)
             finish_cand(N_GROUPS - 1, turn_z(z_t[N_GROUPS - 1]))
             quantise_rows(cand_rows(NODES // P - PACK, PACK), N_PASSES - 1, cand_codes, cand_scales)
             opened = []
@@ -358,9 +386,10 @@ def tile_dgggl_pa_kernel(tc, xg_gate, gate_w_z, gate_b_z, xt, state1, state2, su
         held = 3
         products = firsts[0] + firsts[1][:1] + seconds[0][:-held] + firsts[1][1:] + seconds[0][-held:] + seconds[1]
         stores = []
-        for n, (product, p) in enumerate(products):
+        for n, (product, p) in enumerate(products[:-1]):
             if n >= OPENED:
-                give_a_run()
+                if (n - OPENED) % RUN_PRODUCTS == 0:
+                    give_a_run()
                 flush()
             for give in stores:
                 give()
@@ -379,3 +408,4 @@ def tile_dgggl_pa_kernel(tc, xg_gate, gate_w_z, gate_b_z, xt, state1, state2, su
                 stores.append(partial(store, T2[i], b, t2[p][:]))
         for give in stores:
             give()
+        last_product(products[-1][1])

@@ -40,12 +40,18 @@ OPENED = 2
 RAW_BUFS = 6
 SMALL_AFTER = 5
 FIRST_GATING_STEP = 4
-LAST_STEP_BANKS = 6
+LAST_STEP_BANKS = 8
 FIRST_A_STEP = 7
 A_BANKS_PER_STEP = 3
+TURN_BANKS = 4
+V_BANK = 2
+V_XG = 0
+FLUSH_XG = 1
+FLUSH_A = 0
+Z_POS = 2
 RUN_BANKS = 4
 RUN_PRODUCTS = 1
-GATE_RUN = 3
+GATE_RUN = 4
 
 FLOPS = 2 * NODES * F_GATE * P + 2 * SUPPORTS * 2 * NODES * NODES * C
 
@@ -117,10 +123,10 @@ def tile_dgggl_pa_kernel(tc, xg_gate, gate_w_z, gate_b_z, xt, state1, state2, su
             load_next()
             w_sb = gate_pool.tile([P, F_CHUNKS, PAIR * P], BF16)
             nc.sync.dma_start(out=w_sb[:], in_=gate_w_z.rearrange("(j q e) c -> q j (e c)", q=P, e=PAIR))
+            load_next()
             bias_bf = gate_pool.tile([P, 1], BF16)
             with nc.allow_non_contiguous_dma(reason="128 bias values, one to a partition"):
                 nc.sync.dma_start(out=bias_bf[:], in_=gate_b_z.rearrange("(c o) -> c o", o=1))
-            load_next()
             load_next()
             while len(raw) < SMALL_AFTER:
                 load_next()
@@ -133,17 +139,14 @@ def tile_dgggl_pa_kernel(tc, xg_gate, gate_w_z, gate_b_z, xt, state1, state2, su
             while len(raw) < RAW_BUFS:
                 load_next()
 
-            bias = gate_pool.tile([P, 1], F32)
-            nc.vector.tensor_copy(out=bias[:], in_=bias_bf[:])
-
             def turn_bank():
-                return psum.tile([P, BANK], F32, name="turn_bank", tag="turn_bank", bufs=4)
+                return psum.tile([P, BANK], F32, name="turn_bank", tag="turn_bank", bufs=TURN_BANKS)
 
             def sum_bank():
-                return psum.tile([P, BANK], F32, name="sum_bank", tag="sum_bank", bufs=4)
+                return psum.tile([P, BANK], F32, name="sum_bank", tag="sum_bank", bufs=8 - TURN_BANKS)
 
-            def empty_bank(position, dst, src):
-                if position == 0:
+            def empty_bank(position, dst, src, vector=0):
+                if position == vector:
                     nc.vector.tensor_copy(out=dst, in_=src)
                 else:
                     nc.scalar.copy(out=dst, in_=src)
@@ -158,7 +161,7 @@ def tile_dgggl_pa_kernel(tc, xg_gate, gate_w_z, gate_b_z, xt, state1, state2, su
                 for s in range(PER_BANK):
                     col = (bank_no * PER_BANK + s) * P
                     nc.tensor.transpose(bank[:, s * P : (s + 1) * P], words[:, col : col + P], ident[:])
-                empty_bank(bank_no, xg_t[k][:].bitcast(F32)[:, bank_no * BANK : (bank_no + 1) * BANK], bank[:])
+                empty_bank(bank_no, xg_t[k][:].bitcast(F32)[:, bank_no * BANK : (bank_no + 1) * BANK], bank[:], V_XG)
                 if bank_no == XG_BANKS - 1:
                     load_next()
 
@@ -177,6 +180,7 @@ def tile_dgggl_pa_kernel(tc, xg_gate, gate_w_z, gate_b_z, xt, state1, state2, su
                     bank_no,
                     a_t_words[:, bank_no * PAIR : (bank_no + 1) * PAIR, :, :],
                     bank[:].rearrange("p (x u r) -> p x r u", u=PAIR, r=P),
+                    V_BANK,
                 )
                 if bank_no == A_BANKS - 1:
                     load_next()
@@ -195,7 +199,7 @@ def tile_dgggl_pa_kernel(tc, xg_gate, gate_w_z, gate_b_z, xt, state1, state2, su
 
             def sigmoid(acc):
                 z_t = gate_pool.tile([P, GROUP], F32, name="z_t", tag="z_t", bufs=4)
-                nc.scalar.activation(out=z_t[:], in_=acc[:, 0:GROUP], func=ACT.Sigmoid, bias=bias[:, 0:1], scale=1.0)
+                nc.scalar.activation(out=z_t[:], in_=acc[:, 0:GROUP], func=ACT.Sigmoid, bias=bias_bf[:, 0:1], scale=1.0)
                 return z_t
 
             def turn_z(z_t):
@@ -348,15 +352,16 @@ def tile_dgggl_pa_kernel(tc, xg_gate, gate_w_z, gate_b_z, xt, state1, state2, su
                 if multiplying:
                     acc = sum_bank()
                 for n, bank in enumerate(banks):
-                    if k == 1:
-                        gate_matmuls(acc, k - 1, n * GATE_MATMULS // len(banks), (n + 1) * GATE_MATMULS // len(banks))
+                    if k == 1 and n == 0:
+                        gate_matmuls(acc, k - 1, 0, GATE_MATMULS)
                     bank()
-                    if n == 1:
+                    if n == FLUSH_XG:
                         flush()
+                    if n == Z_POS:
                         z = [turn_z(z_t[group]) for group in gating]
                     if k > 1:
                         gate_matmuls(acc, k - 1, n * GATE_MATMULS // len(banks), (n + 1) * GATE_MATMULS // len(banks))
-                    if n == 2:
+                    if n == min(Z_POS + 1, len(banks) - 1):
                         for group, z_group in zip(gating, z):
                             finish_cand(group, z_group)
                 if multiplying:
@@ -367,9 +372,9 @@ def tile_dgggl_pa_kernel(tc, xg_gate, gate_w_z, gate_b_z, xt, state1, state2, su
                         pending.append(partial(quantise_rows, cand_rows(g * PACK, PACK), g, cand_codes, cand_scales))
             def give_a_run(banks=RUN_BANKS):
                 for n in range(banks):
-                    turn_a()
-                    if n == 0:
+                    if n == FLUSH_A:
                         flush()
+                    turn_a()
 
             give_a_run(GATE_RUN)
             finish_cand(N_GROUPS - 1, turn_z(z_t[N_GROUPS - 1]))

@@ -43,6 +43,10 @@ FIRST_GATING_STEP = 4
 LAST_STEP_BANKS = 8
 FIRST_A_STEP = 7
 A_BANKS_PER_STEP = 3
+LINE = 256
+SCALES_AT = 64
+MOVING_AT = 128
+MOVING_SCALES_AT = 192
 TURN_BANKS = 4
 V_BANK = 2
 V_XG = 0
@@ -69,18 +73,23 @@ def tile_dgggl_pa_kernel(tc, xg_gate, gate_w_z, gate_b_z, xt, state1, state2, su
         psum = ctx.enter_context(tc.psum_pool(name="psum", bufs=1))
         ctx.enter_context(tc.manual_schedule())
 
-        ident = keep.tile([P, P], F32)
-        make_identity(nc, ident[:])
+        def placed(pool, width, dtype, size, start, name, bufs=1):
+            pad = start // size
+            tile = pool.tile([P, pad + width], dtype, name=name, tag=name, bufs=bufs, align_bytes=LINE)
+            return tile[:, pad : pad + width]
+
+        ident = placed(keep, P, F32, 4, MOVING_AT, "ident")
+        make_identity(nc, ident)
         table_warmer = keep.tile([P, 1], F32)
         nc.scalar.activation(out=table_warmer[:], in_=ident[:, 0:1], func=ACT.Sigmoid)
 
-        cand_codes = keep.tile([P, N_PASSES, C], U32, align_bytes=64)
-        cand_scales = keep.tile([P, N_PASSES, C], U8, align_bytes=64)
+        cand_codes = placed(keep, N_PASSES * C, U32, 4, MOVING_AT, "cand_codes")
+        cand_scales = placed(keep, N_PASSES * C, U8, 1, MOVING_SCALES_AT, "cand_scales")
         t1_codes = []
         t1_scales = []
         for i in range(SUPPORTS):
-            t1_codes.append(keep.tile([P, N_PASSES, C], U32, name="t1_codes_%d" % i, align_bytes=64))
-            t1_scales.append(keep.tile([P, N_PASSES, C], U8, name="t1_scales_%d" % i, align_bytes=64))
+            t1_codes.append(placed(keep, N_PASSES * C, U32, 4, MOVING_AT, "t1_codes_%d" % i))
+            t1_scales.append(placed(keep, N_PASSES * C, U8, 1, MOVING_SCALES_AT, "t1_scales_%d" % i))
         cand_t1 = keep.tile([P, N_GROUPS * PAIR, 2 * C], F32)
         t1_last = keep.tile([P, N_GROUPS * PAIR, C], F32)
 
@@ -113,7 +122,7 @@ def tile_dgggl_pa_kernel(tc, xg_gate, gate_w_z, gate_b_z, xt, state1, state2, su
                     return
                 kind, k = sources[n]
                 width = PAIR * (F_GATE if kind == 0 else NODES)
-                tile_n = work.tile([P, width], BF16, name="raw_%d" % n, tag="raw", bufs=RAW_BUFS, align_bytes=64)
+                tile_n = work.tile([P, width], BF16, name="raw_%d" % n, tag="raw", bufs=RAW_BUFS, align_bytes=LINE)
                 i, b = divmod(k, N_GROUPS)
                 for part in range(FIRST_PARTS if n == 0 else 1):
                     cols = slice(part * width // FIRST_PARTS, (part + 1) * width // FIRST_PARTS) if n == 0 else slice(0, width)
@@ -121,8 +130,10 @@ def tile_dgggl_pa_kernel(tc, xg_gate, gate_w_z, gate_b_z, xt, state1, state2, su
                 raw[(kind, k)] = tile_n
 
             load_next()
-            w_sb = gate_pool.tile([P, F_CHUNKS, PAIR * P], BF16)
-            nc.sync.dma_start(out=w_sb[:], in_=gate_w_z.rearrange("(j q e) c -> q j (e c)", q=P, e=PAIR))
+            w_sb = placed(gate_pool, F_CHUNKS * PAIR * P, BF16, 2, MOVING_AT, "w_sb")
+            nc.sync.dma_start(
+                out=w_sb.rearrange("q (j c) -> q j c", j=F_CHUNKS), in_=gate_w_z.rearrange("(j q e) c -> q j (e c)", q=P, e=PAIR)
+            )
             load_next()
             bias_bf = gate_pool.tile([P, 1], BF16)
             with nc.allow_non_contiguous_dma(reason="128 bias values, one to a partition"):
@@ -155,12 +166,12 @@ def tile_dgggl_pa_kernel(tc, xg_gate, gate_w_z, gate_b_z, xt, state1, state2, su
 
             def transpose_xg_bank(k, bank_no):
                 if bank_no == 0:
-                    xg_t[k] = gate_pool.tile([P, F_CHUNKS * GROUP * PAIR], BF16, name="xg_t", tag="xg_t", bufs=2)
+                    xg_t[k] = gate_pool.tile([P, F_CHUNKS * GROUP * PAIR], BF16, name="xg_t", tag="xg_t", bufs=2, align_bytes=LINE)
                 words = raw[(0, k)][:].bitcast(F32)
                 bank = turn_bank()
                 for s in range(PER_BANK):
                     col = (bank_no * PER_BANK + s) * P
-                    nc.tensor.transpose(bank[:, s * P : (s + 1) * P], words[:, col : col + P], ident[:])
+                    nc.tensor.transpose(bank[:, s * P : (s + 1) * P], words[:, col : col + P], ident)
                 empty_bank(bank_no, xg_t[k][:].bitcast(F32)[:, bank_no * BANK : (bank_no + 1) * BANK], bank[:], V_XG)
                 if bank_no == XG_BANKS - 1:
                     load_next()
@@ -169,13 +180,13 @@ def tile_dgggl_pa_kernel(tc, xg_gate, gate_w_z, gate_b_z, xt, state1, state2, su
 
             def transpose_a_bank(m, bank_no):
                 if bank_no == 0:
-                    a_t[m] = work.tile([P, PAIR * NODES], BF16, name="a_t", tag="a_t", bufs=3, align_bytes=64)
+                    a_t[m] = work.tile([P, PAIR * NODES], BF16, name="a_t", tag="a_t", bufs=3, align_bytes=LINE)
                 words = raw[(1, m)][:].bitcast(F32)
                 a_t_words = a_t[m][:].bitcast(F32).rearrange("p (x r u) -> p x r u", r=P, u=PAIR)
                 bank = turn_bank()
                 for s in range(PER_BANK):
                     col = (bank_no * PER_BANK + s) * P
-                    nc.tensor.transpose(bank[:, s * P : (s + 1) * P], words[:, col : col + P], ident[:])
+                    nc.tensor.transpose(bank[:, s * P : (s + 1) * P], words[:, col : col + P], ident)
                 empty_bank(
                     bank_no,
                     a_t_words[:, bank_no * PAIR : (bank_no + 1) * PAIR, :, :],
@@ -191,7 +202,7 @@ def tile_dgggl_pa_kernel(tc, xg_gate, gate_w_z, gate_b_z, xt, state1, state2, su
                     j, h = divmod(n, PAIR)
                     nc.tensor.matmul(
                         out=acc[:, 0:GROUP].rearrange("p (e r) -> p e r", e=PAIR),
-                        lhsT=w_sb[:, j, h * P : (h + 1) * P],
+                        lhsT=w_sb[:, (j * PAIR + h) * P : (j * PAIR + h + 1) * P],
                         rhs=halves[:, j, h, :, :],
                         start=(n == 0),
                         stop=(n == GATE_MATMULS - 1),
@@ -205,7 +216,7 @@ def tile_dgggl_pa_kernel(tc, xg_gate, gate_w_z, gate_b_z, xt, state1, state2, su
             def turn_z(z_t):
                 bank = sum_bank()
                 for e in range(PAIR):
-                    nc.tensor.transpose(bank[:, e * P : (e + 1) * P], z_t[:, e * P : (e + 1) * P], ident[:])
+                    nc.tensor.transpose(bank[:, e * P : (e + 1) * P], z_t[:, e * P : (e + 1) * P], ident)
                 return bank[:, 0:GROUP].rearrange("p (e c) -> p e c", e=PAIR)
 
             def finish_cand(k, z):
@@ -225,20 +236,21 @@ def tile_dgggl_pa_kernel(tc, xg_gate, gate_w_z, gate_b_z, xt, state1, state2, su
                 )
 
             def quantise_rows(rows, g, codes, scales):
-                grouped = work.tile([P, C * PACK], BF16, name="rows_grouped", tag="rows_grouped", align_bytes=64)
+                grouped = work.tile([P, C * PACK], BF16, name="rows_grouped", tag="rows_grouped", align_bytes=LINE)
                 nc.vector.tensor_copy(
                     out=grouped[:].rearrange("p (c t) -> p c t", t=PACK), in_=rows.rearrange("p t c -> p c t")
                 )
-                nc.vector.quantize_mx(out=codes[:, g, :].bitcast(FP8X4), scales=scales[:, g, :], in_=grouped[:])
+                cols = slice(g * C, (g + 1) * C)
+                nc.vector.quantize_mx(out=codes[:, cols].bitcast(FP8X4), scales=scales[:, cols], in_=grouped[:])
 
             a_codes = []
             a_scales = []
 
             def quantise_a_group(m):
                 width = PAIR * N_PASSES * P
-                codes = keep.tile([P, width], U32, name="a_codes", tag="a_codes", bufs=12, align_bytes=64)
-                scales = keep.tile([P, width], U8, name="a_scales", tag="a_scales", bufs=12, align_bytes=64)
-                nc.vector.quantize_mx(out=codes[:].bitcast(FP8X4), scales=scales[:], in_=a_t[m][:])
+                codes = placed(keep, width, U32, 4, 0, "a_codes", bufs=12)
+                scales = placed(keep, width, U8, 1, SCALES_AT, "a_scales", bufs=12)
+                nc.vector.quantize_mx(out=codes.bitcast(FP8X4), scales=scales, in_=a_t[m][:])
                 a_codes.append(codes)
                 a_scales.append(scales)
 
@@ -249,8 +261,8 @@ def tile_dgggl_pa_kernel(tc, xg_gate, gate_w_z, gate_b_z, xt, state1, state2, su
                         out=acc,
                         lhsT=a_codes[m][:, cols].bitcast(FP8X4),
                         lhsT_scale=a_scales[m][:, cols],
-                        rhs=rhs_codes[:, g, :].bitcast(FP8X4),
-                        rhs_scale=rhs_scales[:, g, :],
+                        rhs=rhs_codes[:, g * C : (g + 1) * C].bitcast(FP8X4),
+                        rhs_scale=rhs_scales[:, g * C : (g + 1) * C],
                         start=(g == 0),
                         stop=(g == N_PASSES - 1),
                     )

@@ -48,13 +48,13 @@ SCALES_AT = 64
 MOVING_AT = 128
 MOVING_SCALES_AT = 192
 TURN_BANKS = 4
-V_BANK = 2
-V_XG = 0
+V_BANK = (2,)
+V_XG = (0,)
 FLUSH_XG = 1
 FLUSH_A = 0
 Z_POS = 2
-RUN_BANKS = 4
-RUN_PRODUCTS = 1
+RUN_BANKS = 6
+RUN_PRODUCTS = 2
 GATE_RUN = 4
 
 FLOPS = 2 * NODES * F_GATE * P + 2 * SUPPORTS * 2 * NODES * NODES * C
@@ -151,13 +151,13 @@ def tile_dgggl_pa_kernel(tc, xg_gate, gate_w_z, gate_b_z, xt, state1, state2, su
                 load_next()
 
             def turn_bank():
-                return psum.tile([P, BANK], F32, name="turn_bank", tag="turn_bank", bufs=TURN_BANKS)
+                return psum.tile([P, BANK], F32, name="bank", tag="bank", bufs=8)
 
             def sum_bank():
-                return psum.tile([P, BANK], F32, name="sum_bank", tag="sum_bank", bufs=8 - TURN_BANKS)
+                return psum.tile([P, BANK], F32, name="bank", tag="bank", bufs=8)
 
             def empty_bank(position, dst, src, vector=0):
-                if position == vector:
+                if position in vector:
                     nc.vector.tensor_copy(out=dst, in_=src)
                 else:
                     nc.scalar.copy(out=dst, in_=src)

from contextlib import ExitStack
from functools import partial

import concourse.mybir as mybir
from concourse.masks import make_identity

F32 = mybir.dt.float32
BF16 = mybir.dt.bfloat16
U32 = mybir.dt.uint32
U8 = mybir.dt.uint8
FP8X4 = mybir.dt.float8_e4m3fn_x4
ACT = mybir.ActivationFunctionType
ALU = mybir.AluOpType

P = 128
PAIR = 2
PACK = 4
NODES = 2048
GROUP = P * PAIR
N_GROUPS = NODES // GROUP
N_PASSES = NODES // (P * PACK)
GROUPS_PER_PASS = P * PACK // GROUP
SUPPORTS = 2
F_GATE = 1536
F_CHUNKS = F_GATE // GROUP
D_IN = 128
D_STATE = 64
C = D_IN + 2 * D_STATE
BANK = 512
PER_BANK = BANK // P
A_BANKS = NODES // BANK
GATE_MATMULS = F_CHUNKS * PAIR
XG_BANKS = F_CHUNKS * PAIR // PER_BANK
CAND = 0
T1 = (1, 4)
T2 = (2, 5)

FIRST_PARTS = 2
OPENED = 2
RAW_BUFS = 6
SMALL_AFTER = 5
FIRST_GATING_STEP = 4
LAST_STEP_BANKS = 8
FIRST_A_STEP = 7
A_BANKS_PER_STEP = 3
LINE = 256
SCALES_AT = 64
MOVING_AT = 128
MOVING_SCALES_AT = 192
TURN_BANKS = 4
V_BANK = (2,)
V_XG = (0,)
FLUSH_XG = 1
FLUSH_A = 0
Z_POS = 2
RUN_BANKS = 6
RUN_PRODUCTS = 2
GATE_RUN = 4

FLOPS = 2 * NODES * F_GATE * P + 2 * SUPPORTS * 2 * NODES * NODES * C


def tile_dgggl_pa_kernel(tc, xg_gate, gate_w_z, gate_b_z, xt, state1, state2, supports, out):
    nc = tc.nc

    xg_groups = xg_gate[0].rearrange("(g r e) f -> g r (e f)", r=P, e=PAIR)
    a_groups = [supports[i, 0].rearrange("(g r e) m -> g r (e m)", r=P, e=PAIR) for i in range(SUPPORTS)]
    out_groups = out[0].rearrange("(g r e) f -> g r e f", r=P, e=PAIR)

    with ExitStack() as ctx:
        keep = ctx.enter_context(tc.tile_pool(name="keep", bufs=1))
        work = ctx.enter_context(tc.tile_pool(name="work", bufs=2))
        psum = ctx.enter_context(tc.psum_pool(name="psum", bufs=1))
        ctx.enter_context(tc.manual_schedule())

        def placed(pool, width, dtype, size, start, name, bufs=1):
            pad = start // size
            tile = pool.tile([P, pad + width], dtype, name=name, tag=name, bufs=bufs, align_bytes=LINE)
            return tile[:, pad : pad + width]

        ident = placed(keep, P, F32, 4, MOVING_AT, "ident")
        make_identity(nc, ident)
        table_warmer = keep.tile([P, 1], F32)
        nc.scalar.activation(out=table_warmer[:], in_=ident[:, 0:1], func=ACT.Sigmoid)

        cand_codes = placed(keep, N_PASSES * C, U32, 4, MOVING_AT, "cand_codes")
        cand_scales = placed(keep, N_PASSES * C, U8, 1, MOVING_SCALES_AT, "cand_scales")
        t1_codes = []
        t1_scales = []
        for i in range(SUPPORTS):
            t1_codes.append(placed(keep, N_PASSES * C, U32, 4, MOVING_AT, "t1_codes_%d" % i))
            t1_scales.append(placed(keep, N_PASSES * C, U8, 1, MOVING_SCALES_AT, "t1_scales_%d" % i))
        cand_t1 = keep.tile([P, N_GROUPS * PAIR, 2 * C], F32)
        t1_last = keep.tile([P, N_GROUPS * PAIR, C], F32)

        def cand_rows(first_block, n_blocks):
            return cand_t1[:, first_block : first_block + n_blocks, 0:C]

        def t1_rows(i, first_block, n_blocks):
            if i == 0:
                return cand_t1[:, first_block : first_block + n_blocks, C : 2 * C]
            return t1_last[:, first_block : first_block + n_blocks, :]

        def store(first_term, b, rows):
            col = first_term * C
            nc.sync.dma_start(out=out_groups[b][:, :, col : col + rows.shape[2]], in_=rows)

        with tc.tile_pool(name="gate_pool", bufs=1) as gate_pool:
            sources = []
            m = 0
            for k in range(N_GROUPS):
                sources.append((0, k))
                while m < SUPPORTS * N_GROUPS and m * A_BANKS < (k + 1 - FIRST_A_STEP) * A_BANKS_PER_STEP:
                    sources.append((1, m))
                    m += 1
            sources.extend([(1, later) for later in range(m, SUPPORTS * N_GROUPS)])
            raw = {}

            def load_next():
                n = len(raw)
                if n == len(sources):
                    return
                kind, k = sources[n]
                width = PAIR * (F_GATE if kind == 0 else NODES)
                tile_n = work.tile([P, width], BF16, name="raw_%d" % n, tag="raw", bufs=RAW_BUFS, align_bytes=LINE)
                i, b = divmod(k, N_GROUPS)
                for part in range(FIRST_PARTS if n == 0 else 1):
                    cols = slice(part * width // FIRST_PARTS, (part + 1) * width // FIRST_PARTS) if n == 0 else slice(0, width)
                    nc.sync.dma_start(out=tile_n[:, cols], in_=(xg_groups[k] if kind == 0 else a_groups[i][b])[:, cols])
                raw[(kind, k)] = tile_n

            load_next()
            w_sb = placed(gate_pool, F_CHUNKS * PAIR * P, BF16, 2, MOVING_AT, "w_sb")
            nc.sync.dma_start(
                out=w_sb.rearrange("q (j c) -> q j c", j=F_CHUNKS), in_=gate_w_z.rearrange("(j q e) c -> q j (e c)", q=P, e=PAIR)
            )
            load_next()
            bias_bf = gate_pool.tile([P, 1], BF16)
            with nc.allow_non_contiguous_dma(reason="128 bias values, one to a partition"):
                nc.sync.dma_start(out=bias_bf[:], in_=gate_b_z.rearrange("(c o) -> c o", o=1))
            load_next()
            while len(raw) < SMALL_AFTER:
                load_next()
            xt_sb = gate_pool.tile([P, N_GROUPS, PAIR * D_IN], BF16)
            nc.sync.dma_start(out=xt_sb[:], in_=xt[0].rearrange("(g r e) c -> r g (e c)", r=P, e=PAIR))
            s1_sb = gate_pool.tile([P, N_GROUPS, PAIR * D_STATE], BF16)
            nc.sync.dma_start(out=s1_sb[:], in_=state1[0].rearrange("(g r e) c -> r g (e c)", r=P, e=PAIR))
            s2_sb = gate_pool.tile([P, N_GROUPS, PAIR * D_STATE], BF16)
            nc.sync.dma_start(out=s2_sb[:], in_=state2[0].rearrange("(g r e) c -> r g (e c)", r=P, e=PAIR))
            while len(raw) < RAW_BUFS:
                load_next()

            def turn_bank():
                return psum.tile([P, BANK], F32, name="bank", tag="bank", bufs=8)

            def sum_bank():
                return psum.tile([P, BANK], F32, name="bank", tag="bank", bufs=8)

            def empty_bank(position, dst, src, vector=0):
                if position in vector:
                    nc.vector.tensor_copy(out=dst, in_=src)
                else:
                    nc.scalar.copy(out=dst, in_=src)

            xg_t = {}

            def transpose_xg_bank(k, bank_no):
                if bank_no == 0:
                    xg_t[k] = gate_pool.tile([P, F_CHUNKS * GROUP * PAIR], BF16, name="xg_t", tag="xg_t", bufs=2, align_bytes=LINE)
                words = raw[(0, k)][:].bitcast(F32)
                bank = turn_bank()
                for s in range(PER_BANK):
                    col = (bank_no * PER_BANK + s) * P
                    nc.tensor.transpose(bank[:, s * P : (s + 1) * P], words[:, col : col + P], ident)
                empty_bank(bank_no, xg_t[k][:].bitcast(F32)[:, bank_no * BANK : (bank_no + 1) * BANK], bank[:], V_XG)
                if bank_no == XG_BANKS - 1:
                    load_next()

            a_t = {}

            def transpose_a_bank(m, bank_no):
                if bank_no == 0:
                    a_t[m] = work.tile([P, PAIR * NODES], BF16, name="a_t", tag="a_t", bufs=3, align_bytes=LINE)
                words = raw[(1, m)][:].bitcast(F32)
                a_t_words = a_t[m][:].bitcast(F32).rearrange("p (x r u) -> p x r u", r=P, u=PAIR)
                bank = turn_bank()
                for s in range(PER_BANK):
                    col = (bank_no * PER_BANK + s) * P
                    nc.tensor.transpose(bank[:, s * P : (s + 1) * P], words[:, col : col + P], ident)
                empty_bank(
                    bank_no,
                    a_t_words[:, bank_no * PAIR : (bank_no + 1) * PAIR, :, :],
                    bank[:].rearrange("p (x u r) -> p x r u", u=PAIR, r=P),
                    V_BANK,
                )
                if bank_no == A_BANKS - 1:
                    load_next()

            def gate_matmuls(acc, k, first, last):
                halves = xg_t[k][:].rearrange("p (e j r h) -> p j h e r", e=PAIR, j=F_CHUNKS, h=PAIR)
                for n in range(first, last):
                    j, h = divmod(n, PAIR)
                    nc.tensor.matmul(
                        out=acc[:, 0:GROUP].rearrange("p (e r) -> p e r", e=PAIR),
                        lhsT=w_sb[:, (j * PAIR + h) * P : (j * PAIR + h + 1) * P],
                        rhs=halves[:, j, h, :, :],
                        start=(n == 0),
                        stop=(n == GATE_MATMULS - 1),
                    )

            def sigmoid(acc):
                z_t = gate_pool.tile([P, GROUP], F32, name="z_t", tag="z_t", bufs=4)
                nc.scalar.activation(out=z_t[:], in_=acc[:, 0:GROUP], func=ACT.Sigmoid, bias=bias_bf[:, 0:1], scale=1.0)
                return z_t

            def turn_z(z_t):
                bank = sum_bank()
                for e in range(PAIR):
                    nc.tensor.transpose(bank[:, e * P : (e + 1) * P], z_t[:, e * P : (e + 1) * P], ident)
                return bank[:, 0:GROUP].rearrange("p (e c) -> p e c", e=PAIR)

            def finish_cand(k, z):
                rows = cand_rows(k * PAIR, PAIR)
                nc.scalar.copy(out=rows[:, :, 0:D_IN], in_=xt_sb[:, k, :].rearrange("p (e c) -> p e c", e=PAIR))
                nc.vector.tensor_tensor(
                    out=rows[:, :, D_IN : D_IN + D_STATE],
                    in0=z[:, :, 0:D_STATE],
                    in1=s1_sb[:, k, :].rearrange("p (e c) -> p e c", e=PAIR),
                    op=ALU.mult,
                )
                nc.vector.tensor_tensor(
                    out=rows[:, :, D_IN + D_STATE : C],
                    in0=z[:, :, D_STATE : 2 * D_STATE],
                    in1=s2_sb[:, k, :].rearrange("p (e c) -> p e c", e=PAIR),
                    op=ALU.mult,
                )

            def quantise_rows(rows, g, codes, scales):
                grouped = work.tile([P, C * PACK], BF16, name="rows_grouped", tag="rows_grouped", align_bytes=LINE)
                nc.vector.tensor_copy(
                    out=grouped[:].rearrange("p (c t) -> p c t", t=PACK), in_=rows.rearrange("p t c -> p c t")
                )
                cols = slice(g * C, (g + 1) * C)
                nc.vector.quantize_mx(out=codes[:, cols].bitcast(FP8X4), scales=scales[:, cols], in_=grouped[:])

            a_codes = []
            a_scales = []

            def quantise_a_group(m):
                width = PAIR * N_PASSES * P
                codes = placed(keep, width, U32, 4, 0, "a_codes", bufs=12)
                scales = placed(keep, width, U8, 1, SCALES_AT, "a_scales", bufs=12)
                nc.vector.quantize_mx(out=codes.bitcast(FP8X4), scales=scales, in_=a_t[m][:])
                a_codes.append(codes)
                a_scales.append(scales)

            def multiply(acc, m, e, passes, rhs_codes, rhs_scales):
                for g in passes:
                    cols = slice((e * N_PASSES + g) * P, (e * N_PASSES + g + 1) * P)
                    nc.tensor.matmul_mx(
                        out=acc,
                        lhsT=a_codes[m][:, cols].bitcast(FP8X4),
                        lhsT_scale=a_scales[m][:, cols],
                        rhs=rhs_codes[:, g * C : (g + 1) * C].bitcast(FP8X4),
                        rhs_scale=rhs_scales[:, g * C : (g + 1) * C],
                        start=(g == 0),
                        stop=(g == N_PASSES - 1),
                    )

            def product_with_a(m, rhs_codes, rhs_scales):
                acc = sum_bank()
                for e in range(PAIR):
                    multiply(acc[:, e * C : (e + 1) * C], m, e, range(N_PASSES), rhs_codes, rhs_scales)
                return acc[:].rearrange("p (e c) -> p e c", e=PAIR)

            def first_product(m):
                i, b = divmod(m, N_GROUPS)
                acc = product_with_a(m, cand_codes, cand_scales)
                nc.scalar.copy(out=t1_rows(i, b * PAIR, PAIR), in_=acc)

            def open_first_product(m):
                accs = []
                for e in range(PAIR):
                    accs.append(sum_bank()[:, 0:C])
                    multiply(accs[e], m, e, range(N_PASSES - 1), cand_codes, cand_scales)
                return accs

            def close_first_product(m, accs):
                i, b = divmod(m, N_GROUPS)
                for e in range(PAIR):
                    multiply(accs[e], m, e, range(N_PASSES - 1, N_PASSES), cand_codes, cand_scales)
                    nc.scalar.copy(out=t1_rows(i, b * PAIR + e, 1)[:, 0, :], in_=accs[e])

            def quantise_t1(m):
                i, b = divmod(m, N_GROUPS)
                g, u = divmod(b, GROUPS_PER_PASS)
                if u == GROUPS_PER_PASS - 1:
                    quantise_rows(t1_rows(i, g * PACK, PACK), g, t1_codes[i], t1_scales[i])

            t2 = []

            def second_product(m):
                i, b = divmod(m, N_GROUPS)
                acc = product_with_a(m, t1_codes[i], t1_scales[i])
                width = C * PAIR if i == 0 else C
                rows = late.tile([P, PAIR, width], F32, name="t2_%d" % i, tag="t2_%d" % i, bufs=4)
                if i == 0:
                    nc.scalar.copy(out=rows[:, :, C : 2 * C], in_=cand_rows(b * PAIR, PAIR))
                nc.vector.scalar_tensor_tensor(
                    out=rows[:, :, 0:C],
                    in0=acc,
                    scalar=2.0,
                    in1=cand_rows(b * PAIR, PAIR),
                    op0=ALU.mult,
                    op1=ALU.subtract,
                )
                t2.append(rows)

            def last_product(m):
                i, b = divmod(m, N_GROUPS)
                rows = late.tile([P, PAIR, C], F32, name="t2_%d" % i, tag="t2_%d" % i, bufs=4)
                for e in range(PAIR):
                    acc = sum_bank()[:, 0:C]
                    multiply(acc, m, e, range(N_PASSES), t1_codes[i], t1_scales[i])
                    nc.vector.scalar_tensor_tensor(
                        out=rows[:, e, :],
                        in0=acc,
                        scalar=2.0,
                        in1=cand_rows(b * PAIR + e, 1)[:, 0, :],
                        op0=ALU.mult,
                        op1=ALU.subtract,
                    )
                    nc.sync.dma_start(out=out_groups[b][:, e, T2[i] * C : (T2[i] + 1) * C], in_=rows[:, e, :])

            pending = []

            def flush():
                while pending:
                    pending.pop(0)()

            a_banks = [(m, bank_no) for m in range(SUPPORTS * N_GROUPS) for bank_no in range(A_BANKS)]

            def turn_a():
                if a_banks:
                    m, bank_no = a_banks.pop(0)
                    transpose_a_bank(m, bank_no)
                    if bank_no == A_BANKS - 1:
                        pending.append(partial(quantise_a_group, m))

            z_t = {}
            gated = 0
            for k in range(N_GROUPS + 1):
                banks = []
                if k < N_GROUPS:
                    banks.extend([partial(transpose_xg_bank, k, bank_no) for bank_no in range(XG_BANKS)])
                if k >= FIRST_A_STEP:
                    for n in range(A_BANKS_PER_STEP if k < N_GROUPS else LAST_STEP_BANKS):
                        banks.insert(min(2 * n + 1, len(banks)), turn_a)
                gating = []
                while k >= FIRST_GATING_STEP and len(gating) < 2 and gated < k - 1:
                    gating.append(gated)
                    gated += 1
                multiplying = 0 <= k - 1
                if multiplying:
                    acc = sum_bank()
                for n, bank in enumerate(banks):
                    if k == 1 and n == 0:
                        gate_matmuls(acc, k - 1, 0, GATE_MATMULS)
                    bank()
                    if n == FLUSH_XG:
                        flush()
                    if n == Z_POS:
                        z = [turn_z(z_t[group]) for group in gating]
                    if k > 1:
                        gate_matmuls(acc, k - 1, n * GATE_MATMULS // len(banks), (n + 1) * GATE_MATMULS // len(banks))
                    if n == min(Z_POS + 1, len(banks) - 1):
                        for group, z_group in zip(gating, z):
                            finish_cand(group, z_group)
                if multiplying:
                    z_t[k - 1] = sigmoid(acc)
                for group in gating:
                    g, u = divmod(group, GROUPS_PER_PASS)
                    if u == GROUPS_PER_PASS - 1:
                        pending.append(partial(quantise_rows, cand_rows(g * PACK, PACK), g, cand_codes, cand_scales))
            def give_a_run(banks=RUN_BANKS):
                for n in range(banks):
                    if n == FLUSH_A:
                        flush()
                    turn_a()

            give_a_run(GATE_RUN)
            finish_cand(N_GROUPS - 1, turn_z(z_t[N_GROUPS - 1]))
            quantise_rows(cand_rows(NODES // P - PACK, PACK), N_PASSES - 1, cand_codes, cand_scales)
            opened = []
            for m in range(OPENED):
                opened.append(open_first_product(m))
                if m < OPENED - 1:
                    give_a_run()

        late = ctx.enter_context(tc.tile_pool(name="late", bufs=1))
        firsts = [[(first_product, i * N_GROUPS + b) for b in range(N_GROUPS)] for i in range(SUPPORTS)]
        seconds = [[(second_product, i * N_GROUPS + b) for b in range(N_GROUPS)] for i in range(SUPPORTS)]
        held = 3
        products = firsts[0] + firsts[1][:1] + seconds[0][:-held] + firsts[1][1:] + seconds[0][-held:] + seconds[1]
        stores = []
        for n, (product, p) in enumerate(products[:-1]):
            if n >= OPENED:
                if (n - OPENED) % RUN_PRODUCTS == 0:
                    give_a_run()
                flush()
            for give in stores:
                give()
            stores = []
            if n < OPENED:
                close_first_product(p, opened[p])
            else:
                product(p)
            i, b = divmod(p, N_GROUPS)
            if product is first_product:
                if b % GROUPS_PER_PASS == GROUPS_PER_PASS - 1:
                    pending.append(partial(quantise_t1, p))
                rows = cand_t1[:, b * PAIR : (b + 1) * PAIR, :] if i == 0 else t1_rows(i, b * PAIR, PAIR)
                stores.append(partial(store, CAND if i == 0 else T1[i], b, rows))
            else:
                stores.append(partial(store, T2[i], b, t2[p][:]))
        for give in stores:
            give()
        last_product(products[-1][1])
